import numpy as np
import ml_dtypes


def mxq(x, axis, fmt="e4m3"):
    dtype, down = {"e4m3": (ml_dtypes.float8_e4m3fn, 7), "e5m2": (ml_dtypes.float8_e5m2, 14)}[fmt]
    v = np.moveaxis(np.asarray(x, np.float32).astype(ml_dtypes.bfloat16).astype(np.float64), axis, -1)
    blocks = v.reshape(v.shape[:-1] + (-1, 32))
    amax = np.abs(blocks).max(-1, keepdims=True)
    byte = np.maximum(np.where(amax > 0, np.frexp(amax)[1] - 1 + 127, 0) - down, 1)
    scale = np.exp2(byte - 127.0)
    codes = (blocks / scale).astype(np.float32).astype(dtype).astype(np.float64)
    return np.moveaxis((codes * scale).reshape(v.shape), -1, axis)


WIDE = False


def mx_kscale(k):
    if not WIDE:
        return np.ones(k)
    levels = np.array([10, -10, 5, -5, 0])
    a = np.random.permutation(np.resize(levels, k // 512 * 4)).reshape(k // 512, 4)
    idx = np.arange(k)
    return np.exp2(a[idx // 512, idx % 128 // 32])


BF16 = ml_dtypes.bfloat16


def bf(x):
    return np.asarray(x, np.float32).astype(BF16)


def f64(x):
    return np.asarray(x).astype(np.float64)


N, IN_F, HID, OUT_F = 1024, 512, 8192, 512


def setup_inputs():
    s = mx_kscale(HID)
    g = 0.1 + 0.9 * np.random.random_sample(N)
    adj = np.random.random_sample((N, N)) * g[:, None] * g[None, :]
    return {"h1": bf(np.random.standard_normal((N, HID)) * s),
            "adj": bf(adj),
            "W2": bf(np.random.standard_normal((OUT_F, HID)) * 0.125 * np.sqrt(N / HID) / s[None, :]),
            "b2": bf(np.random.standard_normal(OUT_F) * 0.1)}


def reference(h1, adj, W2, b2):
    h = (mxq(f64(h1), 1, "e4m3") @ mxq(f64(W2), 1, "e4m3").T) + f64(b2)
    A = f64(adj) + np.eye(N)
    rowsum = A.sum(axis=1)
    r_inv_sqrt = np.power(rowsum, -0.5)
    r_inv_sqrt = np.where(np.isinf(r_inv_sqrt), 0.0, r_inv_sqrt)
    A = r_inv_sqrt[:, None] * A * r_inv_sqrt[None, :]
    return mxq(A, 1, "e4m3") @ mxq(h, 0, "e4m3")

@@ -1,0 +1,306 @@
+from contextlib import ExitStack
+
+import concourse.mybir as mybir
+from concourse.masks import make_identity
+
+F32 = mybir.dt.float32
+BF16 = mybir.dt.bfloat16
+U32 = mybir.dt.uint32
+U8 = mybir.dt.uint8
+FP8X4 = mybir.dt.float8_e4m3fn_x4
+ACT = mybir.ActivationFunctionType
+ALU = mybir.AluOpType
+
+P = 128
+PACK = 4
+K_PASS = P * PACK
+NODES, HID, OUT_F = 1024, 8192, 512
+PASSES = HID // K_PASS
+NODE_TILES = NODES // P
+NODE_PASSES = NODES // K_PASS
+HALF_TILES = NODE_TILES // 2
+UNIT_WORDS = K_PASS // 2
+RAW_K = 4096
+SLAB_K = RAW_K // HALF_TILES
+ROUNDS_A = PASSES
+ROUNDS = ROUNDS_A + 2 * HALF_TILES
+PAIRS = ROUNDS // 2
+PAIRS_AHEAD = 3
+
+FLOPS = 2 * NODES * HID * OUT_F + 2 * NODES * NODES * OUT_F
+
+
+def tile_gcnlayer_pa_k_kernel(tc, h1, adj, W2, b2, out):
+    nc = tc.nc
+    with ExitStack() as ctx:
+        ctx.enter_context(tc.manual_schedule())
+        keep = ctx.enter_context(tc.tile_pool(name="keep", bufs=1))
+        raw_pool = ctx.enter_context(tc.tile_pool(name="raw", bufs=2 * (PAIRS_AHEAD + 1)))
+        stage = ctx.enter_context(tc.tile_pool(name="stage", bufs=4))
+        tr_psum = ctx.enter_context(tc.psum_pool(name="tr_psum", bufs=4))
+        acc_psum = ctx.enter_context(tc.psum_pool(name="acc_psum", bufs=4))
+
+        ident_f32 = keep.tile([P, P], F32)
+        make_identity(nc, ident_f32[:])
+        ident_bf16 = keep.tile([P, P], BF16)
+        make_identity(nc, ident_bf16[:])
+
+        one = keep.tile([P, 1], F32)
+        nc.vector.memset(one[:], 1.0)
+        one_root = keep.tile([P, 1], F32)
+        nc.scalar.activation(out=one_root[:], in_=one[:], func=ACT.Sqrt)
+
+        w_codes = keep.tile([P, PASSES, OUT_F], U32, align_bytes=64)
+        w_scales = keep.tile([P, PASSES, OUT_F], U8, align_bytes=64)
+        bias_bc = keep.tile([P, OUT_F], BF16)
+        h_bf16 = keep.tile([P, NODE_TILES, OUT_F], BF16)
+        h_grouped = keep.tile([P, NODE_PASSES, OUT_F * PACK], BF16, align_bytes=64)
+        h_codes = keep.tile([P, NODE_PASSES, OUT_F], U32, align_bytes=64)
+        h_scales = keep.tile([P, NODE_PASSES, OUT_F], U8, align_bytes=64)
+        adj_sb = keep.tile([P, NODE_TILES, NODES], BF16)
+        adj_copy = keep.tile([P, NODES], BF16)
+        diag = keep.tile([P, NODE_TILES, P], F32)
+        adj_sum = keep.tile([P, NODE_TILES], F32)
+        r_bc = keep.tile([P, NODES], F32)
+        an_codes = keep.tile([P, NODE_TILES, NODE_PASSES * P], U32, align_bytes=64)
+        an_scales = keep.tile([P, NODE_TILES, NODE_PASSES * P], U8, align_bytes=64)
+
+        raw = {}
+
+        def load_pair(pair):
+            first = raw_pool.tile([P, RAW_K], BF16, tag="raw")
+            second = raw_pool.tile([P, RAW_K], BF16, tag="raw")
+            if pair < ROUNDS_A // 2:
+                k_cols = slice(pair * SLAB_K, (pair + 1) * SLAB_K)
+                nc.sync.dma_start(
+                    out=first[:].rearrange("p (a k) -> p a k", a=HALF_TILES),
+                    in_=W2[:, k_cols].rearrange("(a p) k -> p a k", p=P),
+                )
+                nc.sync.dma_start(
+                    out=second[:].rearrange("p (a k) -> p a k", a=HALF_TILES),
+                    in_=h1[0 : HALF_TILES * P, k_cols].rearrange("(a p) k -> p a k", p=P),
+                )
+                nc.sync.dma_start(out=adj_sb[:, pair, :], in_=adj[pair * P : (pair + 1) * P, :])
+            else:
+                m = pair - ROUNDS_A // 2 + HALF_TILES
+                if m == HALF_TILES:
+                    nc.sync.dma_start(out=bias_bc[:], in_=b2.partition_broadcast(P))
+                nc.sync.dma_start(out=first[:], in_=h1[m * P : (m + 1) * P, 0:RAW_K])
+                nc.sync.dma_start(out=second[:], in_=h1[m * P : (m + 1) * P, RAW_K : 2 * RAW_K])
+            raw[pair] = (first, second)
+
+        def copy_out(on_vector, dst, src):
+            if on_vector:
+                nc.vector.tensor_copy(out=dst, in_=src)
+            else:
+                nc.scalar.copy(out=dst, in_=src)
+
+        def transpose_four_units(raw_tile, word_offsets, bank_on_vector):
+            words = raw_tile[:].bitcast(F32)
+            grouped = stage.tile([P, PACK * K_PASS], BF16, tag="grouped", align_bytes=64)
+            grouped_words = grouped[:].bitcast(F32).rearrange("p (n r u) -> p n r u", n=4, u=2)
+            for b in range(2):
+                bank = tr_psum.tile([P, 2, 2, P], F32, tag="bank")
+                for n in range(2):
+                    for u in range(2):
+                        col = word_offsets[2 * b + n] + u * P
+                        nc.tensor.transpose(bank[:, n, u, :], words[:, col : col + P], ident_f32[:])
+                copy_out(
+                    bank_on_vector[b],
+                    grouped_words[:, 2 * b : 2 * b + 2],
+                    bank[:].rearrange("p n u r -> p n r u"),
+                )
+            return grouped
+
+        def quantise(grouped, codes, scales):
+            nc.vector.quantize_mx(out=codes.bitcast(FP8X4), scales=scales, in_=grouped)
+
+        def new_x_codes():
+            x_codes = stage.tile([P, PACK * P], U32, tag="x_codes", align_bytes=64)
+            x_scales = stage.tile([P, PACK * P], U8, tag="x_scales", align_bytes=64)
+            return x_codes, x_scales
+
+        acc = {}
+
+        def run_passes(passes):
+            for m, c, x_codes, x_scales in passes:
+                if c == 0:
+                    acc[m] = acc_psum.tile([P, OUT_F], F32, tag="acc", name="acc%d" % m)
+                nc.tensor.matmul_mx(
+                    out=acc[m][:],
+                    lhsT=x_codes.bitcast(FP8X4),
+                    lhsT_scale=x_scales,
+                    rhs=w_codes[:, c, :].bitcast(FP8X4),
+                    rhs_scale=w_scales[:, c, :],
+                    start=(c == 0),
+                    stop=(c == PASSES - 1),
+                )
+
+        def h_from_sums(m):
+            nc.vector.tensor_tensor(out=h_bf16[:, m, :], in0=acc[m][:], in1=bias_bc[:], op=ALU.add)
+
+        def group_h(g):
+            nc.vector.tensor_copy(
+                out=h_grouped[:, g, :].rearrange("p (f t) -> p f t", t=PACK),
+                in_=h_bf16[:, PACK * g : PACK * (g + 1), :].rearrange("p t f -> p f t"),
+            )
+
+        def quantise_h(g):
+            quantise(h_grouped[:, g, :], h_codes[:, g, :], h_scales[:, g, :])
+
+        an_rows = {}
+        an_grouped = {}
+
+        def adj_row_sum(a):
+            nc.scalar.activation(
+                out=adj_copy[:], in_=adj_sb[:, a, :], func=ACT.Copy, accum_out=adj_sum[:, a : a + 1]
+            )
+            nc.vector.tensor_tensor(
+                out=diag[:, a, :], in0=adj_sb[:, a, a * P : (a + 1) * P], in1=ident_bf16[:], op=ALU.add
+            )
+
+        def adj_scale(a):
+            rows = stage.tile([P, NODES], BF16, tag="an_rows")
+            block = slice(a * P, (a + 1) * P)
+            nc.vector.scalar_tensor_tensor(
+                out=rows[:], in0=adj_sb[:, a, :], scalar=r[:, a : a + 1], in1=r_bc[:],
+                op0=ALU.mult, op1=ALU.mult,
+            )
+            nc.vector.scalar_tensor_tensor(
+                out=rows[:, block], in0=diag[:, a, :], scalar=r[:, a : a + 1], in1=r_bc[:, block],
+                op0=ALU.mult, op1=ALU.mult,
+            )
+            an_rows[a] = rows
+
+        def adj_transpose(a):
+            an_t = acc_psum.tile([P, NODE_TILES, P], BF16, tag="acc")
+            for jt in range(NODE_TILES):
+                nc.tensor.transpose(an_t[:, jt, :], an_rows[a][:, jt * P : (jt + 1) * P], ident_bf16[:])
+            grouped = stage.tile([P, NODE_PASSES * K_PASS], BF16, tag="an_grouped", align_bytes=64)
+            nc.scalar.copy(
+                out=grouped[:].rearrange("p (g i t) -> p g i t", g=NODE_PASSES, t=PACK),
+                in_=an_t[:].rearrange("p (g t) i -> p g i t", t=PACK),
+            )
+            an_grouped[a] = grouped
+
+        def adj_quantise(a):
+            quantise(an_grouped[a][:], an_codes[:, a, :], an_scales[:, a, :])
+
+        for pair in range(PAIRS_AHEAD):
+            load_pair(pair)
+        waiting = []
+        for c in range(ROUNDS_A):
+            if c % 2 == 0:
+                load_pair(c // 2 + PAIRS_AHEAD)
+            w_raw, x_raw = raw[c // 2]
+            offsets = [a * 2 * UNIT_WORDS + (c % 2) * UNIT_WORDS for a in range(HALF_TILES)]
+            sums_adj = c % 2 == 1
+            w_grouped = transpose_four_units(w_raw, offsets, (False, sums_adj))
+            x_grouped = transpose_four_units(x_raw, offsets, (False, True))
+            quantise(w_grouped[:], w_codes[:, c, :], w_scales[:, c, :])
+            x_codes, x_scales = new_x_codes()
+            quantise(x_grouped[:], x_codes[:], x_scales[:])
+            if sums_adj:
+                adj_row_sum(c // 2)
+            run_passes(waiting)
+            waiting = []
+            for m in range(HALF_TILES):
+                cols = slice(m * P, (m + 1) * P)
+                waiting.append((m, c, x_codes[:, cols], x_scales[:, cols]))
+
+        deg = keep.tile([P, NODE_TILES], F32)
+        nc.vector.tensor_scalar_add(out=deg[:], in0=adj_sum[:], scalar1=1.0)
+        root = keep.tile([P, NODE_TILES], F32)
+        nc.scalar.activation(out=root[:], in_=deg[:], func=ACT.Sqrt)
+        r_first = keep.tile([P, NODE_TILES], F32)
+        nc.vector.reciprocal(out=r_first[:], in_=root[:])
+        deg_rr = keep.tile([P, NODE_TILES], F32)
+        nc.vector.tensor_tensor(out=deg_rr[:], in0=deg[:], in1=r_first[:], op=ALU.mult)
+        nc.vector.tensor_tensor(out=deg_rr[:], in0=deg_rr[:], in1=r_first[:], op=ALU.mult)
+        nc.vector.tensor_scalar(
+            out=deg_rr[:], in0=deg_rr[:], scalar1=-0.5, scalar2=1.5, op0=ALU.mult, op1=ALU.add
+        )
+        r = keep.tile([P, NODE_TILES], F32)
+        nc.vector.tensor_tensor(out=r[:], in0=r_first[:], in1=deg_rr[:], op=ALU.mult)
+
+        def spread_r():
+            for half in range(2):
+                bank = tr_psum.tile([P, PACK, P], F32, tag="bank")
+                for q in range(PACK):
+                    a = PACK * half + q
+                    nc.tensor.transpose(bank[:, q, :], r[:, a : a + 1].to_broadcast([P, P]), ident_f32[:])
+                nc.scalar.copy(
+                    out=r_bc[:, half * K_PASS : (half + 1) * K_PASS],
+                    in_=bank[:].rearrange("p q c -> p (q c)"),
+                )
+
+        for i in range(ROUNDS_A, ROUNDS):
+            if i % 2 == 0 and i // 2 + PAIRS_AHEAD < PAIRS:
+                load_pair(i // 2 + PAIRS_AHEAD)
+            m = (i - ROUNDS_A) // 2 + HALF_TILES
+            a_scale = i - ROUNDS_A - 1
+            a_pack = a_scale - 1
+            if a_scale == 0:
+                spread_r()
+            x_raw = raw[i // 2][i % 2]
+            grouped = []
+            for call in range(2):
+                offsets = [(PACK * call + n) * UNIT_WORDS for n in range(PACK)]
+                grouped.append(transpose_four_units(x_raw, offsets, (False, False)))
+            if a_pack >= 0:
+                adj_transpose(a_pack)
+            fresh = []
+            for call in range(2):
+                x_codes, x_scales = new_x_codes()
+                quantise(grouped[call][:], x_codes[:], x_scales[:])
+                for n in range(PACK):
+                    cols = slice(n * P, (n + 1) * P)
+                    c = (i % 2) * 2 * PACK + PACK * call + n
+                    fresh.append((m, c, x_codes[:, cols], x_scales[:, cols]))
+                if call == 0 and a_scale >= 0:
+                    adj_scale(a_scale)
+            if a_pack >= 0:
+                adj_quantise(a_pack)
+            run_passes(waiting)
+            waiting = fresh
+            if i == ROUNDS_A:
+                for done in range(HALF_TILES):
+                    h_from_sums(done)
+                group_h(0)
+                quantise_h(0)
+            elif i % 2 == 0:
+                h_from_sums(m - 1)
+
+        adj_transpose(NODE_TILES - 2)
+        adj_scale(NODE_TILES - 1)
+        adj_quantise(NODE_TILES - 2)
+        run_passes(waiting)
+        adj_transpose(NODE_TILES - 1)
+        h_from_sums(NODE_TILES - 1)
+        group_h(1)
+        adj_quantise(NODE_TILES - 1)
+        quantise_h(1)
+
+        out_sums = []
+        for a in range(NODE_TILES):
+            if a < HALF_TILES:
+                out_sum = tr_psum.tile([P, OUT_F], F32, tag="bank")
+            else:
+                out_sum = acc_psum.tile([P, OUT_F], F32, tag="acc")
+            out_sums.append(out_sum)
+        for g in range(NODE_PASSES):
+            for a in range(NODE_TILES):
+                cols = slice(g * P, (g + 1) * P)
+                nc.tensor.matmul_mx(
+                    out=out_sums[a][:],
+                    lhsT=an_codes[:, a, cols].bitcast(FP8X4),
+                    lhsT_scale=an_scales[:, a, cols],
+                    rhs=h_codes[:, g, :].bitcast(FP8X4),
+                    rhs_scale=h_scales[:, g, :],
+                    start=(g == 0),
+                    stop=(g == NODE_PASSES - 1),
+                )
+        for a in range(NODE_TILES):
+            out_sb = stage.tile([P, OUT_F], F32, tag="out_sb")
+            copy_out(a % 2 == 1, out_sb[:], out_sums[a][:])
+            nc.sync.dma_start(out=out[a * P : (a + 1) * P, :], in_=out_sb[:])

@@ -26,6 +26,7 @@ ROUNDS_A = PASSES
 ROUNDS = ROUNDS_A + 2 * HALF_TILES
 PAIRS = ROUNDS // 2
 PAIRS_AHEAD = 3
+MX_LAG = 2
 
 FLOPS = 2 * NODES * HID * OUT_F + 2 * NODES * NODES * OUT_F
 
@@ -58,9 +59,9 @@ def tile_gcnlayer_pa_k_kernel(tc, h1, adj, W2, b2, out):
         h_codes = keep.tile([P, NODE_PASSES, OUT_F], U32, align_bytes=64)
         h_scales = keep.tile([P, NODE_PASSES, OUT_F], U8, align_bytes=64)
         adj_sb = keep.tile([P, NODE_TILES, NODES], BF16)
-        adj_copy = keep.tile([P, NODES], BF16)
+        adj_copy = keep.tile([P, NODES // 2], BF16)
         diag = keep.tile([P, NODE_TILES, P], F32)
-        adj_sum = keep.tile([P, NODE_TILES], F32)
+        adj_sum = keep.tile([P, NODE_TILES, 2], F32)
         r_bc = keep.tile([P, NODES], F32)
         an_codes = keep.tile([P, NODE_TILES, NODE_PASSES * P], U32, align_bytes=64)
         an_scales = keep.tile([P, NODE_TILES, NODE_PASSES * P], U8, align_bytes=64)
@@ -116,14 +117,16 @@ def tile_gcnlayer_pa_k_kernel(tc, h1, adj, W2, b2, out):
             nc.vector.quantize_mx(out=codes.bitcast(FP8X4), scales=scales, in_=grouped)
 
         def new_x_codes():
-            x_codes = stage.tile([P, PACK * P], U32, tag="x_codes", align_bytes=64)
-            x_scales = stage.tile([P, PACK * P], U8, tag="x_scales", align_bytes=64)
+            alive = 2 * (MX_LAG + 1)
+            x_codes = stage.tile([P, PACK * P], U32, tag="x_codes", bufs=alive, align_bytes=64)
+            x_scales = stage.tile([P, PACK * P], U8, tag="x_scales", bufs=alive, align_bytes=64)
             return x_codes, x_scales
 
         acc = {}
+        passes_of_round = {}
 
-        def run_passes(passes):
-            for m, c, x_codes, x_scales in passes:
+        def run_passes(done_round):
+            for m, c, x_codes, x_scales in passes_of_round[done_round]:
                 if c == 0:
                     acc[m] = acc_psum.tile([P, OUT_F], F32, tag="acc", name="acc%d" % m)
                 nc.tensor.matmul_mx(
@@ -148,13 +151,30 @@ def tile_gcnlayer_pa_k_kernel(tc, h1, adj, W2, b2, out):
         def quantise_h(g):
             quantise(h_grouped[:, g, :], h_codes[:, g, :], h_scales[:, g, :])
 
+        def finish_node_tiles(done_round):
+            closed = []
+            if done_round == ROUNDS_A - 1:
+                closed = list(range(HALF_TILES))
+            elif done_round >= ROUNDS_A and done_round % 2 == 1:
+                closed = [(done_round - ROUNDS_A) // 2 + HALF_TILES]
+            for m in closed:
+                h_from_sums(m)
+                if m % PACK == PACK - 1:
+                    group_h(m // PACK)
+                    quantise_h(m // PACK)
+
         an_rows = {}
         an_grouped = {}
 
-        def adj_row_sum(a):
+        def adj_half_row_sum(a, s):
             nc.scalar.activation(
-                out=adj_copy[:], in_=adj_sb[:, a, :], func=ACT.Copy, accum_out=adj_sum[:, a : a + 1]
+                out=adj_copy[:],
+                in_=adj_sb[:, a, s * (NODES // 2) : (s + 1) * (NODES // 2)],
+                func=ACT.Copy,
+                accum_out=adj_sum[:, a, s : s + 1],
             )
+
+        def adj_add_identity(a):
             nc.vector.tensor_tensor(
                 out=diag[:, a, :], in0=adj_sb[:, a, a * P : (a + 1) * P], in1=ident_bf16[:], op=ALU.add
             )
@@ -188,28 +208,30 @@ def tile_gcnlayer_pa_k_kernel(tc, h1, adj, W2, b2, out):
 
         for pair in range(PAIRS_AHEAD):
             load_pair(pair)
-        waiting = []
         for c in range(ROUNDS_A):
             if c % 2 == 0:
                 load_pair(c // 2 + PAIRS_AHEAD)
             w_raw, x_raw = raw[c // 2]
             offsets = [a * 2 * UNIT_WORDS + (c % 2) * UNIT_WORDS for a in range(HALF_TILES)]
-            sums_adj = c % 2 == 1
-            w_grouped = transpose_four_units(w_raw, offsets, (False, sums_adj))
+            w_grouped = transpose_four_units(w_raw, offsets, (False, False))
             x_grouped = transpose_four_units(x_raw, offsets, (False, True))
             quantise(w_grouped[:], w_codes[:, c, :], w_scales[:, c, :])
             x_codes, x_scales = new_x_codes()
             quantise(x_grouped[:], x_codes[:], x_scales[:])
-            if sums_adj:
-                adj_row_sum(c // 2)
-            run_passes(waiting)
-            waiting = []
-            for m in range(HALF_TILES):
-                cols = slice(m * P, (m + 1) * P)
-                waiting.append((m, c, x_codes[:, cols], x_scales[:, cols]))
+            adj_half_row_sum(c // 2, c % 2)
+            if c % 2 == 1:
+                adj_add_identity(c // 2)
+            passes_of_round[c] = [
+                (m, c, x_codes[:, m * P : (m + 1) * P], x_scales[:, m * P : (m + 1) * P])
+                for m in range(HALF_TILES)
+            ]
+            if c >= MX_LAG:
+                run_passes(c - MX_LAG)
 
         deg = keep.tile([P, NODE_TILES], F32)
-        nc.vector.tensor_scalar_add(out=deg[:], in0=adj_sum[:], scalar1=1.0)
+        nc.vector.scalar_tensor_tensor(
+            out=deg[:], in0=adj_sum[:, :, 0], scalar=1.0, in1=adj_sum[:, :, 1], op0=ALU.add, op1=ALU.add
+        )
         root = keep.tile([P, NODE_TILES], F32)
         nc.scalar.activation(out=root[:], in_=deg[:], func=ACT.Sqrt)
         r_first = keep.tile([P, NODE_TILES], F32)
@@ -234,52 +256,41 @@ def tile_gcnlayer_pa_k_kernel(tc, h1, adj, W2, b2, out):
                     in_=bank[:].rearrange("p q c -> p (q c)"),
                 )
 
-        for i in range(ROUNDS_A, ROUNDS):
+        for i in range(ROUNDS_A, ROUNDS + MX_LAG):
             if i % 2 == 0 and i // 2 + PAIRS_AHEAD < PAIRS:
                 load_pair(i // 2 + PAIRS_AHEAD)
-            m = (i - ROUNDS_A) // 2 + HALF_TILES
             a_scale = i - ROUNDS_A - 1
             a_pack = a_scale - 1
             if a_scale == 0:
                 spread_r()
-            x_raw = raw[i // 2][i % 2]
             grouped = []
-            for call in range(2):
-                offsets = [(PACK * call + n) * UNIT_WORDS for n in range(PACK)]
-                grouped.append(transpose_four_units(x_raw, offsets, (False, False)))
-            if a_pack >= 0:
+            if i < ROUNDS:
+                for call in range(2):
+                    offsets = [(PACK * call + n) * UNIT_WORDS for n in range(PACK)]
+                    grouped.append(transpose_four_units(raw[i // 2][i % 2], offsets, (False, False)))
+            if 0 <= a_pack:
                 adj_transpose(a_pack)
-            fresh = []
-            for call in range(2):
+            passes_of_round[i] = []
+            for call in range(len(grouped)):
                 x_codes, x_scales = new_x_codes()
                 quantise(grouped[call][:], x_codes[:], x_scales[:])
                 for n in range(PACK):
-                    cols = slice(n * P, (n + 1) * P)
-                    c = (i % 2) * 2 * PACK + PACK * call + n
-                    fresh.append((m, c, x_codes[:, cols], x_scales[:, cols]))
-                if call == 0 and a_scale >= 0:
+                    passes_of_round[i].append(
+                        (
+                            (i - ROUNDS_A) // 2 + HALF_TILES,
+                            (i % 2) * 2 * PACK + PACK * call + n,
+                            x_codes[:, n * P : (n + 1) * P],
+                            x_scales[:, n * P : (n + 1) * P],
+                        )
+                    )
+                if call == 0 and 0 <= a_scale:
                     adj_scale(a_scale)
-            if a_pack >= 0:
+            if i >= ROUNDS and a_scale < NODE_TILES:
+                adj_scale(a_scale)
+            if 0 <= a_pack:
                 adj_quantise(a_pack)
-            run_passes(waiting)
-            waiting = fresh
-            if i == ROUNDS_A:
-                for done in range(HALF_TILES):
-                    h_from_sums(done)
-                group_h(0)
-                quantise_h(0)
-            elif i % 2 == 0:
-                h_from_sums(m - 1)
-
-        adj_transpose(NODE_TILES - 2)
-        adj_scale(NODE_TILES - 1)
-        adj_quantise(NODE_TILES - 2)
-        run_passes(waiting)
-        adj_transpose(NODE_TILES - 1)
-        h_from_sums(NODE_TILES - 1)
-        group_h(1)
-        adj_quantise(NODE_TILES - 1)
-        quantise_h(1)
+            run_passes(i - MX_LAG)
+            finish_node_tiles(i - MX_LAG)
 
         out_sums = []
         for a in range(NODE_TILES):

@@ -26,7 +26,6 @@ ROUNDS_A = PASSES
 ROUNDS = ROUNDS_A + 2 * HALF_TILES
 PAIRS = ROUNDS // 2
 PAIRS_AHEAD = 3
-MX_LAG = 2
 
 FLOPS = 2 * NODES * HID * OUT_F + 2 * NODES * NODES * OUT_F
 
@@ -59,9 +58,9 @@ def tile_gcnlayer_pa_k_kernel(tc, h1, adj, W2, b2, out):
         h_codes = keep.tile([P, NODE_PASSES, OUT_F], U32, align_bytes=64)
         h_scales = keep.tile([P, NODE_PASSES, OUT_F], U8, align_bytes=64)
         adj_sb = keep.tile([P, NODE_TILES, NODES], BF16)
-        adj_copy = keep.tile([P, NODES // 2], BF16)
+        adj_copy = keep.tile([P, NODES], BF16)
         diag = keep.tile([P, NODE_TILES, P], F32)
-        adj_sum = keep.tile([P, NODE_TILES, 2], F32)
+        adj_sum = keep.tile([P, NODE_TILES], F32)
         r_bc = keep.tile([P, NODES], F32)
         an_codes = keep.tile([P, NODE_TILES, NODE_PASSES * P], U32, align_bytes=64)
         an_scales = keep.tile([P, NODE_TILES, NODE_PASSES * P], U8, align_bytes=64)
@@ -117,16 +116,14 @@ def tile_gcnlayer_pa_k_kernel(tc, h1, adj, W2, b2, out):
             nc.vector.quantize_mx(out=codes.bitcast(FP8X4), scales=scales, in_=grouped)
 
         def new_x_codes():
-            alive = 2 * (MX_LAG + 1)
-            x_codes = stage.tile([P, PACK * P], U32, tag="x_codes", bufs=alive, align_bytes=64)
-            x_scales = stage.tile([P, PACK * P], U8, tag="x_scales", bufs=alive, align_bytes=64)
+            x_codes = stage.tile([P, PACK * P], U32, tag="x_codes", align_bytes=64)
+            x_scales = stage.tile([P, PACK * P], U8, tag="x_scales", align_bytes=64)
             return x_codes, x_scales
 
         acc = {}
-        passes_of_round = {}
 
-        def run_passes(done_round):
-            for m, c, x_codes, x_scales in passes_of_round[done_round]:
+        def run_passes(passes):
+            for m, c, x_codes, x_scales in passes:
                 if c == 0:
                     acc[m] = acc_psum.tile([P, OUT_F], F32, tag="acc", name="acc%d" % m)
                 nc.tensor.matmul_mx(
@@ -151,30 +148,13 @@ def tile_gcnlayer_pa_k_kernel(tc, h1, adj, W2, b2, out):
         def quantise_h(g):
             quantise(h_grouped[:, g, :], h_codes[:, g, :], h_scales[:, g, :])
 
-        def finish_node_tiles(done_round):
-            closed = []
-            if done_round == ROUNDS_A - 1:
-                closed = list(range(HALF_TILES))
-            elif done_round >= ROUNDS_A and done_round % 2 == 1:
-                closed = [(done_round - ROUNDS_A) // 2 + HALF_TILES]
-            for m in closed:
-                h_from_sums(m)
-                if m % PACK == PACK - 1:
-                    group_h(m // PACK)
-                    quantise_h(m // PACK)
-
         an_rows = {}
         an_grouped = {}
 
-        def adj_half_row_sum(a, s):
+        def adj_row_sum(a):
             nc.scalar.activation(
-                out=adj_copy[:],
-                in_=adj_sb[:, a, s * (NODES // 2) : (s + 1) * (NODES // 2)],
-                func=ACT.Copy,
-                accum_out=adj_sum[:, a, s : s + 1],
+                out=adj_copy[:], in_=adj_sb[:, a, :], func=ACT.Copy, accum_out=adj_sum[:, a : a + 1]
             )
-
-        def adj_add_identity(a):
             nc.vector.tensor_tensor(
                 out=diag[:, a, :], in0=adj_sb[:, a, a * P : (a + 1) * P], in1=ident_bf16[:], op=ALU.add
             )
@@ -208,30 +188,28 @@ def tile_gcnlayer_pa_k_kernel(tc, h1, adj, W2, b2, out):
 
         for pair in range(PAIRS_AHEAD):
             load_pair(pair)
+        waiting = []
         for c in range(ROUNDS_A):
             if c % 2 == 0:
                 load_pair(c // 2 + PAIRS_AHEAD)
             w_raw, x_raw = raw[c // 2]
             offsets = [a * 2 * UNIT_WORDS + (c % 2) * UNIT_WORDS for a in range(HALF_TILES)]
-            w_grouped = transpose_four_units(w_raw, offsets, (False, False))
+            sums_adj = c % 2 == 1
+            w_grouped = transpose_four_units(w_raw, offsets, (False, sums_adj))
             x_grouped = transpose_four_units(x_raw, offsets, (False, True))
             quantise(w_grouped[:], w_codes[:, c, :], w_scales[:, c, :])
             x_codes, x_scales = new_x_codes()
             quantise(x_grouped[:], x_codes[:], x_scales[:])
-            adj_half_row_sum(c // 2, c % 2)
-            if c % 2 == 1:
-                adj_add_identity(c // 2)
-            passes_of_round[c] = [
-                (m, c, x_codes[:, m * P : (m + 1) * P], x_scales[:, m * P : (m + 1) * P])
-                for m in range(HALF_TILES)
-            ]
-            if c >= MX_LAG:
-                run_passes(c - MX_LAG)
+            if sums_adj:
+                adj_row_sum(c // 2)
+            run_passes(waiting)
+            waiting = []
+            for m in range(HALF_TILES):
+                cols = slice(m * P, (m + 1) * P)
+                waiting.append((m, c, x_codes[:, cols], x_scales[:, cols]))
 
         deg = keep.tile([P, NODE_TILES], F32)
-        nc.vector.scalar_tensor_tensor(
-            out=deg[:], in0=adj_sum[:, :, 0], scalar=1.0, in1=adj_sum[:, :, 1], op0=ALU.add, op1=ALU.add
-        )
+        nc.vector.tensor_scalar_add(out=deg[:], in0=adj_sum[:], scalar1=1.0)
         root = keep.tile([P, NODE_TILES], F32)
         nc.scalar.activation(out=root[:], in_=deg[:], func=ACT.Sqrt)
         r_first = keep.tile([P, NODE_TILES], F32)
@@ -256,41 +234,52 @@ def tile_gcnlayer_pa_k_kernel(tc, h1, adj, W2, b2, out):
                     in_=bank[:].rearrange("p q c -> p (q c)"),
                 )
 
-        for i in range(ROUNDS_A, ROUNDS + MX_LAG):
+        for i in range(ROUNDS_A, ROUNDS):
             if i % 2 == 0 and i // 2 + PAIRS_AHEAD < PAIRS:
                 load_pair(i // 2 + PAIRS_AHEAD)
+            m = (i - ROUNDS_A) // 2 + HALF_TILES
             a_scale = i - ROUNDS_A - 1
             a_pack = a_scale - 1
             if a_scale == 0:
                 spread_r()
+            x_raw = raw[i // 2][i % 2]
             grouped = []
-            if i < ROUNDS:
-                for call in range(2):
-                    offsets = [(PACK * call + n) * UNIT_WORDS for n in range(PACK)]
-                    grouped.append(transpose_four_units(raw[i // 2][i % 2], offsets, (False, False)))
-            if 0 <= a_pack:
+            for call in range(2):
+                offsets = [(PACK * call + n) * UNIT_WORDS for n in range(PACK)]
+                grouped.append(transpose_four_units(x_raw, offsets, (False, False)))
+            if a_pack >= 0:
                 adj_transpose(a_pack)
-            passes_of_round[i] = []
-            for call in range(len(grouped)):
+            fresh = []
+            for call in range(2):
                 x_codes, x_scales = new_x_codes()
                 quantise(grouped[call][:], x_codes[:], x_scales[:])
                 for n in range(PACK):
-                    passes_of_round[i].append(
-                        (
-                            (i - ROUNDS_A) // 2 + HALF_TILES,
-                            (i % 2) * 2 * PACK + PACK * call + n,
-                            x_codes[:, n * P : (n + 1) * P],
-                            x_scales[:, n * P : (n + 1) * P],
-                        )
-                    )
-                if call == 0 and 0 <= a_scale:
+                    cols = slice(n * P, (n + 1) * P)
+                    c = (i % 2) * 2 * PACK + PACK * call + n
+                    fresh.append((m, c, x_codes[:, cols], x_scales[:, cols]))
+                if call == 0 and a_scale >= 0:
                     adj_scale(a_scale)
-            if i >= ROUNDS and a_scale < NODE_TILES:
-                adj_scale(a_scale)
-            if 0 <= a_pack:
+            if a_pack >= 0:
                 adj_quantise(a_pack)
-            run_passes(i - MX_LAG)
-            finish_node_tiles(i - MX_LAG)
+            run_passes(waiting)
+            waiting = fresh
+            if i == ROUNDS_A:
+                for done in range(HALF_TILES):
+                    h_from_sums(done)
+                group_h(0)
+                quantise_h(0)
+            elif i % 2 == 0:
+                h_from_sums(m - 1)
+
+        adj_transpose(NODE_TILES - 2)
+        adj_scale(NODE_TILES - 1)
+        adj_quantise(NODE_TILES - 2)
+        run_passes(waiting)
+        adj_transpose(NODE_TILES - 1)
+        h_from_sums(NODE_TILES - 1)
+        group_h(1)
+        adj_quantise(NODE_TILES - 1)
+        quantise_h(1)
 
         out_sums = []
         for a in range(NODE_TILES):
@@ -312,6 +301,6 @@ def tile_gcnlayer_pa_k_kernel(tc, h1, adj, W2, b2, out):
                     stop=(g == NODE_PASSES - 1),
                 )
         for a in range(NODE_TILES):
-            out_sb = stage.tile([P, OUT_F], F32, tag="out_sb")
+            out_sb = stage.tile([P, OUT_F], F32, tag="out_sb", bufs=NODE_TILES)
             copy_out(a % 2 == 1, out_sb[:], out_sums[a][:])
             nc.sync.dma_start(out=out[a * P : (a + 1) * P, :], in_=out_sb[:])

@@ -19,6 +19,8 @@ PASSES = HID // K_PASS
 NODE_TILES = NODES // P
 NODE_PASSES = NODES // K_PASS
 HALF_TILES = NODE_TILES // 2
+HALF_F = OUT_F // 2
+LAST = NODE_TILES - 1
 UNIT_WORDS = K_PASS // 2
 RAW_K = 4096
 SLAB_K = RAW_K // HALF_TILES
@@ -26,6 +28,7 @@ ROUNDS_A = PASSES
 ROUNDS = ROUNDS_A + 2 * HALF_TILES
 PAIRS = ROUNDS // 2
 PAIRS_AHEAD = 3
+AN_SCALED = ((), (0,), (1,), (2, 3), (4,), (5, 6), (7,), ())
 
 FLOPS = 2 * NODES * HID * OUT_F + 2 * NODES * NODES * OUT_F
 
@@ -122,31 +125,39 @@ def tile_gcnlayer_pa_k_kernel(tc, h1, adj, W2, b2, out):
 
         acc = {}
 
-        def run_passes(passes):
+        def run_passes(passes, f0=0, width=OUT_F):
             for m, c, x_codes, x_scales in passes:
                 if c == 0:
-                    acc[m] = acc_psum.tile([P, OUT_F], F32, tag="acc", name="acc%d" % m)
+                    acc[m, f0] = acc_psum.tile([P, width], F32, tag="acc", name="acc%d_%d" % (m, f0))
                 nc.tensor.matmul_mx(
-                    out=acc[m][:],
+                    out=acc[m, f0][:],
                     lhsT=x_codes.bitcast(FP8X4),
                     lhsT_scale=x_scales,
-                    rhs=w_codes[:, c, :].bitcast(FP8X4),
-                    rhs_scale=w_scales[:, c, :],
+                    rhs=w_codes[:, c, f0 : f0 + width].bitcast(FP8X4),
+                    rhs_scale=w_scales[:, c, f0 : f0 + width],
                     start=(c == 0),
                     stop=(c == PASSES - 1),
                 )
 
-        def h_from_sums(m):
-            nc.vector.tensor_tensor(out=h_bf16[:, m, :], in0=acc[m][:], in1=bias_bc[:], op=ALU.add)
-
-        def group_h(g):
-            nc.vector.tensor_copy(
-                out=h_grouped[:, g, :].rearrange("p (f t) -> p f t", t=PACK),
-                in_=h_bf16[:, PACK * g : PACK * (g + 1), :].rearrange("p t f -> p f t"),
+        def h_from_sums(m, f0=0, width=OUT_F):
+            features = slice(f0, f0 + width)
+            nc.vector.tensor_tensor(
+                out=h_bf16[:, m, features], in0=acc[m, f0][:], in1=bias_bc[:, features], op=ALU.add
             )
 
-        def quantise_h(g):
-            quantise(h_grouped[:, g, :], h_codes[:, g, :], h_scales[:, g, :])
+        def group_h(g, f0=0, width=OUT_F):
+            nc.vector.tensor_copy(
+                out=h_grouped[:, g, PACK * f0 : PACK * (f0 + width)].rearrange("p (f t) -> p f t", t=PACK),
+                in_=h_bf16[:, PACK * g : PACK * (g + 1), f0 : f0 + width].rearrange("p t f -> p f t"),
+            )
+
+        def quantise_h(g, f0=0, width=OUT_F):
+            features = slice(f0, f0 + width)
+            quantise(
+                h_grouped[:, g, PACK * f0 : PACK * (f0 + width)],
+                h_codes[:, g, features],
+                h_scales[:, g, features],
+            )
 
         an_rows = {}
         an_grouped = {}
@@ -234,21 +245,22 @@ def tile_gcnlayer_pa_k_kernel(tc, h1, adj, W2, b2, out):
                     in_=bank[:].rearrange("p q c -> p (q c)"),
                 )
 
+        last_passes = []
         for i in range(ROUNDS_A, ROUNDS):
             if i % 2 == 0 and i // 2 + PAIRS_AHEAD < PAIRS:
                 load_pair(i // 2 + PAIRS_AHEAD)
             m = (i - ROUNDS_A) // 2 + HALF_TILES
-            a_scale = i - ROUNDS_A - 1
-            a_pack = a_scale - 1
-            if a_scale == 0:
+            to_scale = AN_SCALED[i - ROUNDS_A]
+            to_pack = AN_SCALED[i - ROUNDS_A - 1] if i > ROUNDS_A else ()
+            if i == ROUNDS_A + 1:
                 spread_r()
             x_raw = raw[i // 2][i % 2]
             grouped = []
             for call in range(2):
                 offsets = [(PACK * call + n) * UNIT_WORDS for n in range(PACK)]
                 grouped.append(transpose_four_units(x_raw, offsets, (False, False)))
-            if a_pack >= 0:
-                adj_transpose(a_pack)
+            for a in to_pack:
+                adj_transpose(a)
             fresh = []
             for call in range(2):
                 x_codes, x_scales = new_x_codes()
@@ -257,50 +269,61 @@ def tile_gcnlayer_pa_k_kernel(tc, h1, adj, W2, b2, out):
                     cols = slice(n * P, (n + 1) * P)
                     c = (i % 2) * 2 * PACK + PACK * call + n
                     fresh.append((m, c, x_codes[:, cols], x_scales[:, cols]))
-                if call == 0 and a_scale >= 0:
-                    adj_scale(a_scale)
-            if a_pack >= 0:
-                adj_quantise(a_pack)
-            run_passes(waiting)
+                if call == 0:
+                    for a in to_scale:
+                        adj_scale(a)
+            for a in to_pack:
+                adj_quantise(a)
+            if i < ROUNDS - 1:
+                run_passes(waiting)
+            else:
+                last_passes = waiting + fresh
+                run_passes(waiting, 0, HALF_F)
             waiting = fresh
             if i == ROUNDS_A:
                 for done in range(HALF_TILES):
                     h_from_sums(done)
-                group_h(0)
-                quantise_h(0)
             elif i % 2 == 0:
                 h_from_sums(m - 1)
+            if i == ROUNDS_A + 3:
+                group_h(0)
+            elif i == ROUNDS_A + 5:
+                quantise_h(0)
 
-        adj_transpose(NODE_TILES - 2)
-        adj_scale(NODE_TILES - 1)
-        adj_quantise(NODE_TILES - 2)
-        run_passes(waiting)
-        adj_transpose(NODE_TILES - 1)
-        h_from_sums(NODE_TILES - 1)
-        group_h(1)
-        adj_quantise(NODE_TILES - 1)
-        quantise_h(1)
+        run_passes(waiting, 0, HALF_F)
+        run_passes(last_passes, HALF_F, HALF_F)
 
-        out_sums = []
-        for a in range(NODE_TILES):
-            if a < HALF_TILES:
-                out_sum = tr_psum.tile([P, OUT_F], F32, tag="bank")
-            else:
-                out_sum = acc_psum.tile([P, OUT_F], F32, tag="acc")
-            out_sums.append(out_sum)
-        for g in range(NODE_PASSES):
+        for f0 in (0, HALF_F):
+            h_from_sums(LAST, f0, HALF_F)
+            group_h(1, f0, HALF_F)
+            quantise_h(1, f0, HALF_F)
+
+        out_sb = keep.tile([P, NODE_TILES, OUT_F], F32)
+        for f0 in (0, HALF_F):
+            features = slice(f0, f0 + HALF_F)
+            out_sums = []
             for a in range(NODE_TILES):
-                cols = slice(g * P, (g + 1) * P)
-                nc.tensor.matmul_mx(
-                    out=out_sums[a][:],
-                    lhsT=an_codes[:, a, cols].bitcast(FP8X4),
-                    lhsT_scale=an_scales[:, a, cols],
-                    rhs=h_codes[:, g, :].bitcast(FP8X4),
-                    rhs_scale=h_scales[:, g, :],
-                    start=(g == 0),
-                    stop=(g == NODE_PASSES - 1),
-                )
-        for a in range(NODE_TILES):
-            out_sb = stage.tile([P, OUT_F], F32, tag="out_sb", bufs=NODE_TILES)
-            copy_out(a % 2 == 1, out_sb[:], out_sums[a][:])
-            nc.sync.dma_start(out=out[a * P : (a + 1) * P, :], in_=out_sb[:])
+                if a < HALF_TILES:
+                    out_sum = tr_psum.tile([P, HALF_F], F32, tag="bank")
+                else:
+                    out_sum = acc_psum.tile([P, HALF_F], F32, tag="acc")
+                out_sums.append(out_sum)
+                for g in range(NODE_PASSES):
+                    cols = slice(g * P, (g + 1) * P)
+                    nc.tensor.matmul_mx(
+                        out=out_sum[:],
+                        lhsT=an_codes[:, a, cols].bitcast(FP8X4),
+                        lhsT_scale=an_scales[:, a, cols],
+                        rhs=h_codes[:, g, features].bitcast(FP8X4),
+                        rhs_scale=h_scales[:, g, features],
+                        start=(g == 0),
+                        stop=(g == NODE_PASSES - 1),
+                    )
+            on_vector = (5, 6, 7) if f0 == 0 else (1, 3, 5, 7)
+            for a in range(NODE_TILES):
+                copy_out(a in on_vector, out_sb[:, a, features], out_sums[a][:])
+                if a % 2 == 1:
+                    nc.sync.dma_start(
+                        out=out[(a - 1) * P : (a + 1) * P, features].rearrange("(t p) f -> p t f", p=P),
+                        in_=out_sb[:, a - 1 : a + 1, features],
+                    )

@@ -22,13 +22,20 @@ HALF_TILES = NODE_TILES // 2
 HALF_F = OUT_F // 2
 LAST = NODE_TILES - 1
 UNIT_WORDS = K_PASS // 2
-RAW_K = 4096
-SLAB_K = RAW_K // HALF_TILES
+RAW_UNITS = 4
+RAW_K = RAW_UNITS * K_PASS
+SLAB_PASSES = 2
+SLAB_K = SLAB_PASSES * K_PASS
+SLAB_LOADS = 4
+RAW_BUFS = 20
 ROUNDS_A = PASSES
 ROUNDS = ROUNDS_A + 2 * HALF_TILES
-PAIRS = ROUNDS // 2
-PAIRS_AHEAD = 3
-AN_SCALED = ((), (0,), (1,), (2, 3), (4,), (5, 6), (7,), ())
+LOADS_A = SLAB_LOADS * PASSES // SLAB_PASSES
+TILE_LOADS = PASSES // RAW_UNITS
+LOADS = LOADS_A + HALF_TILES * TILE_LOADS
+ADJ_LOADS = {20: (0,), 22: (1,), 24: (2,), 26: (3,), 28: (4,), 30: (5,), 32: (6, 7)}
+ADJ_SUM_ROUNDS = 8
+AN_SCALED = ((), (), (0,), (1, 2), (3,), (4, 5), (6, 7), ())
 
 FLOPS = 2 * NODES * HID * OUT_F + 2 * NODES * NODES * OUT_F
 
@@ -38,7 +45,7 @@ def tile_gcnlayer_pa_k_kernel(tc, h1, adj, W2, b2, out):
     with ExitStack() as ctx:
         ctx.enter_context(tc.manual_schedule())
         keep = ctx.enter_context(tc.tile_pool(name="keep", bufs=1))
-        raw_pool = ctx.enter_context(tc.tile_pool(name="raw", bufs=2 * (PAIRS_AHEAD + 1)))
+        raw_pool = ctx.enter_context(tc.tile_pool(name="raw", bufs=RAW_BUFS))
         stage = ctx.enter_context(tc.tile_pool(name="stage", bufs=4))
         tr_psum = ctx.enter_context(tc.psum_pool(name="tr_psum", bufs=4))
         acc_psum = ctx.enter_context(tc.psum_pool(name="acc_psum", bufs=4))
@@ -64,33 +71,47 @@ def tile_gcnlayer_pa_k_kernel(tc, h1, adj, W2, b2, out):
         adj_copy = keep.tile([P, NODES], BF16)
         diag = keep.tile([P, NODE_TILES, P], F32)
         adj_sum = keep.tile([P, NODE_TILES], F32)
+        deg = keep.tile([P, NODE_TILES], F32)
+        root = keep.tile([P, NODE_TILES], F32)
+        r_first = keep.tile([P, NODE_TILES], F32)
+        deg_rr = keep.tile([P, NODE_TILES], F32)
+        r = keep.tile([P, NODE_TILES], F32)
         r_bc = keep.tile([P, NODES], F32)
         an_codes = keep.tile([P, NODE_TILES, NODE_PASSES * P], U32, align_bytes=64)
         an_scales = keep.tile([P, NODE_TILES, NODE_PASSES * P], U8, align_bytes=64)
 
-        raw = {}
+        raw = []
+        first_slab = []
 
-        def load_pair(pair):
-            first = raw_pool.tile([P, RAW_K], BF16, tag="raw")
-            second = raw_pool.tile([P, RAW_K], BF16, tag="raw")
-            if pair < ROUNDS_A // 2:
-                k_cols = slice(pair * SLAB_K, (pair + 1) * SLAB_K)
-                nc.sync.dma_start(
-                    out=first[:].rearrange("p (a k) -> p a k", a=HALF_TILES),
-                    in_=W2[:, k_cols].rearrange("(a p) k -> p a k", p=P),
-                )
-                nc.sync.dma_start(
-                    out=second[:].rearrange("p (a k) -> p a k", a=HALF_TILES),
-                    in_=h1[0 : HALF_TILES * P, k_cols].rearrange("(a p) k -> p a k", p=P),
-                )
-                nc.sync.dma_start(out=adj_sb[:, pair, :], in_=adj[pair * P : (pair + 1) * P, :])
-            else:
-                m = pair - ROUNDS_A // 2 + HALF_TILES
-                if m == HALF_TILES:
+        def load_to(end):
+            for n in range(len(raw), min(end, LOADS)):
+                raw_tile = raw_pool.tile([P, RAW_K], BF16, tag="raw")
+                raw.append(raw_tile)
+                if n < LOADS_A:
+                    slab, i = divmod(n, SLAB_LOADS)
+                    src, a = (W2, 2 * i) if i < 2 else (h1, 2 * (i - 2))
+                    rows = src[a * P : (a + 2) * P, slab * SLAB_K : (slab + 1) * SLAB_K]
+                    rows = rows.rearrange("(t p) k -> p t k", p=P)
+                    tile_rows = raw_tile[:].rearrange("p (t k) -> p t k", t=2)
+                    if slab > 0:
+                        nc.sync.dma_start(out=tile_rows, in_=rows)
+                    else:
+                        first_slab.append((tile_rows, rows))
+                    if n == SLAB_LOADS - 1:
+                        for c in range(SLAB_PASSES):
+                            cols = slice(c * K_PASS, (c + 1) * K_PASS)
+                            for dst, src_rows in first_slab:
+                                nc.sync.dma_start(out=dst[:, :, cols], in_=src_rows[:, :, cols])
+                else:
+                    m, q = divmod(n - LOADS_A, TILE_LOADS)
+                    a = HALF_TILES + m
+                    nc.sync.dma_start(
+                        out=raw_tile[:], in_=h1[a * P : (a + 1) * P, q * RAW_K : (q + 1) * RAW_K]
+                    )
+                for b in ADJ_LOADS.get(n + 1, ()):
+                    nc.sync.dma_start(out=adj_sb[:, b, :], in_=adj[b * P : (b + 1) * P, :])
+                if n + 1 == LOADS_A:
                     nc.sync.dma_start(out=bias_bc[:], in_=b2.partition_broadcast(P))
-                nc.sync.dma_start(out=first[:], in_=h1[m * P : (m + 1) * P, 0:RAW_K])
-                nc.sync.dma_start(out=second[:], in_=h1[m * P : (m + 1) * P, RAW_K : 2 * RAW_K])
-            raw[pair] = (first, second)
 
         def copy_out(on_vector, dst, src):
             if on_vector:
@@ -98,15 +119,16 @@ def tile_gcnlayer_pa_k_kernel(tc, h1, adj, W2, b2, out):
             else:
                 nc.scalar.copy(out=dst, in_=src)
 
-        def transpose_four_units(raw_tile, word_offsets, bank_on_vector):
-            words = raw_tile[:].bitcast(F32)
+        def transpose_four_units(units, bank_on_vector):
             grouped = stage.tile([P, PACK * K_PASS], BF16, tag="grouped", align_bytes=64)
             grouped_words = grouped[:].bitcast(F32).rearrange("p (n r u) -> p n r u", n=4, u=2)
             for b in range(2):
                 bank = tr_psum.tile([P, 2, 2, P], F32, tag="bank")
                 for n in range(2):
+                    raw_tile, unit = units[2 * b + n]
+                    words = raw_tile[:].bitcast(F32)
                     for u in range(2):
-                        col = word_offsets[2 * b + n] + u * P
+                        col = unit * UNIT_WORDS + u * P
                         nc.tensor.transpose(bank[:, n, u, :], words[:, col : col + P], ident_f32[:])
                 copy_out(
                     bank_on_vector[b],
@@ -197,42 +219,37 @@ def tile_gcnlayer_pa_k_kernel(tc, h1, adj, W2, b2, out):
         def adj_quantise(a):
             quantise(an_grouped[a][:], an_codes[:, a, :], an_scales[:, a, :])
 
-        for pair in range(PAIRS_AHEAD):
-            load_pair(pair)
         waiting = []
         for c in range(ROUNDS_A):
-            if c % 2 == 0:
-                load_pair(c // 2 + PAIRS_AHEAD)
-            w_raw, x_raw = raw[c // 2]
-            offsets = [a * 2 * UNIT_WORDS + (c % 2) * UNIT_WORDS for a in range(HALF_TILES)]
-            sums_adj = c % 2 == 1
-            w_grouped = transpose_four_units(w_raw, offsets, (False, sums_adj))
-            x_grouped = transpose_four_units(x_raw, offsets, (False, True))
+            slab, in_slab = divmod(c, SLAB_PASSES)
+            used = SLAB_LOADS * slab
+            load_to(used + RAW_BUFS)
+            w_units = [(raw[used + a // 2], SLAB_PASSES * (a % 2) + in_slab) for a in range(HALF_TILES)]
+            x_units = [(raw[used + 2 + a // 2], SLAB_PASSES * (a % 2) + in_slab) for a in range(HALF_TILES)]
+            sums_adj = c >= ADJ_SUM_ROUNDS
+            w_grouped = transpose_four_units(w_units, (False, sums_adj))
+            x_grouped = transpose_four_units(x_units, (False, True))
             quantise(w_grouped[:], w_codes[:, c, :], w_scales[:, c, :])
             x_codes, x_scales = new_x_codes()
             quantise(x_grouped[:], x_codes[:], x_scales[:])
             if sums_adj:
-                adj_row_sum(c // 2)
+                adj_row_sum(c - ADJ_SUM_ROUNDS)
             run_passes(waiting)
             waiting = []
             for m in range(HALF_TILES):
                 cols = slice(m * P, (m + 1) * P)
                 waiting.append((m, c, x_codes[:, cols], x_scales[:, cols]))
 
-        deg = keep.tile([P, NODE_TILES], F32)
-        nc.vector.tensor_scalar_add(out=deg[:], in0=adj_sum[:], scalar1=1.0)
-        root = keep.tile([P, NODE_TILES], F32)
-        nc.scalar.activation(out=root[:], in_=deg[:], func=ACT.Sqrt)
-        r_first = keep.tile([P, NODE_TILES], F32)
-        nc.vector.reciprocal(out=r_first[:], in_=root[:])
-        deg_rr = keep.tile([P, NODE_TILES], F32)
-        nc.vector.tensor_tensor(out=deg_rr[:], in0=deg[:], in1=r_first[:], op=ALU.mult)
-        nc.vector.tensor_tensor(out=deg_rr[:], in0=deg_rr[:], in1=r_first[:], op=ALU.mult)
-        nc.vector.tensor_scalar(
-            out=deg_rr[:], in0=deg_rr[:], scalar1=-0.5, scalar2=1.5, op0=ALU.mult, op1=ALU.add
-        )
-        r = keep.tile([P, NODE_TILES], F32)
-        nc.vector.tensor_tensor(out=r[:], in0=r_first[:], in1=deg_rr[:], op=ALU.mult)
+        def degrees_to_r():
+            nc.vector.tensor_scalar_add(out=deg[:], in0=adj_sum[:], scalar1=1.0)
+            nc.scalar.activation(out=root[:], in_=deg[:], func=ACT.Sqrt)
+            nc.vector.reciprocal(out=r_first[:], in_=root[:])
+            nc.vector.tensor_tensor(out=deg_rr[:], in0=deg[:], in1=r_first[:], op=ALU.mult)
+            nc.vector.tensor_tensor(out=deg_rr[:], in0=deg_rr[:], in1=r_first[:], op=ALU.mult)
+            nc.vector.tensor_scalar(
+                out=deg_rr[:], in0=deg_rr[:], scalar1=-0.5, scalar2=1.5, op0=ALU.mult, op1=ALU.add
+            )
+            nc.vector.tensor_tensor(out=r[:], in0=r_first[:], in1=deg_rr[:], op=ALU.mult)
 
         def spread_r():
             for half in range(2):
@@ -247,18 +264,19 @@ def tile_gcnlayer_pa_k_kernel(tc, h1, adj, W2, b2, out):
 
         last_passes = []
         for i in range(ROUNDS_A, ROUNDS):
-            if i % 2 == 0 and i // 2 + PAIRS_AHEAD < PAIRS:
-                load_pair(i // 2 + PAIRS_AHEAD)
+            used = LOADS_A + 2 * (i - ROUNDS_A)
+            load_to(used + RAW_BUFS)
             m = (i - ROUNDS_A) // 2 + HALF_TILES
             to_scale = AN_SCALED[i - ROUNDS_A]
             to_pack = AN_SCALED[i - ROUNDS_A - 1] if i > ROUNDS_A else ()
-            if i == ROUNDS_A + 1:
-                spread_r()
-            x_raw = raw[i // 2][i % 2]
+            if i == ROUNDS_A:
+                degrees_to_r()
             grouped = []
             for call in range(2):
-                offsets = [(PACK * call + n) * UNIT_WORDS for n in range(PACK)]
-                grouped.append(transpose_four_units(x_raw, offsets, (False, False)))
+                units = [(raw[used + call], n) for n in range(RAW_UNITS)]
+                grouped.append(transpose_four_units(units, (False, False)))
+            if i == ROUNDS_A + 1:
+                spread_r()
             for a in to_pack:
                 adj_transpose(a)
             fresh = []
@@ -285,9 +303,9 @@ def tile_gcnlayer_pa_k_kernel(tc, h1, adj, W2, b2, out):
                     h_from_sums(done)
             elif i % 2 == 0:
                 h_from_sums(m - 1)
-            if i == ROUNDS_A + 3:
+            if i == ROUNDS_A + 1:
                 group_h(0)
-            elif i == ROUNDS_A + 5:
+            elif i == ROUNDS_A + 2:
                 quantise_h(0)
 
         run_passes(waiting, 0, HALF_F)
@@ -298,7 +316,10 @@ def tile_gcnlayer_pa_k_kernel(tc, h1, adj, W2, b2, out):
             group_h(1, f0, HALF_F)
             quantise_h(1, f0, HALF_F)
 
-        out_sb = keep.tile([P, NODE_TILES, OUT_F], F32)
+        out_sb = []
+        for n in range(NODE_TILES // 2):
+            out_pair = raw_pool.tile([P, 2, OUT_F], F32, tag="raw")
+            out_sb.append(out_pair)
         for f0 in (0, HALF_F):
             features = slice(f0, f0 + HALF_F)
             out_sums = []
@@ -321,9 +342,9 @@ def tile_gcnlayer_pa_k_kernel(tc, h1, adj, W2, b2, out):
                     )
             on_vector = (5, 6, 7) if f0 == 0 else (1, 3, 5, 7)
             for a in range(NODE_TILES):
-                copy_out(a in on_vector, out_sb[:, a, features], out_sums[a][:])
+                copy_out(a in on_vector, out_sb[a // 2][:, a % 2, features], out_sums[a][:])
                 if a % 2 == 1:
                     nc.sync.dma_start(
                         out=out[(a - 1) * P : (a + 1) * P, features].rearrange("(t p) f -> p t f", p=P),
-                        in_=out_sb[:, a - 1 : a + 1, features],
+                        in_=out_sb[a // 2][:, :, features],
                     )

@@ -62,7 +62,11 @@ def tile_gcnlayer_pa_k_kernel(tc, h1, adj, W2, b2, out):
 
         w_codes = keep.tile([P, PASSES, OUT_F], U32, align_bytes=64)
         w_scales = keep.tile([P, PASSES, OUT_F], U8, align_bytes=64)
-        bias_bc = keep.tile([P, OUT_F], BF16)
+        bias_row = keep.tile([P, OUT_F], BF16)
+        nc.vector.memset(bias_row[:], 0.0)
+        ones = keep.tile([P, P], BF16)
+        nc.vector.memset(ones[:], 1.0)
+        bias_bc = keep.tile([P, OUT_F], F32)
         h_bf16 = keep.tile([P, NODE_TILES, OUT_F], BF16)
         h_grouped = keep.tile([P, NODE_PASSES, OUT_F * PACK], BF16, align_bytes=64)
         h_codes = keep.tile([P, NODE_PASSES, OUT_F], U32, align_bytes=64)
@@ -91,7 +95,7 @@ def tile_gcnlayer_pa_k_kernel(tc, h1, adj, W2, b2, out):
                     slab, i = divmod(n, SLAB_LOADS)
                     src, a = (W2, 2 * i) if i < 2 else (h1, 2 * (i - 2))
                     rows = src[a * P : (a + 2) * P, slab * SLAB_K : (slab + 1) * SLAB_K]
-                    rows = rows.rearrange("(t p) k -> p t k", p=P)
+                    rows = rows.rearrange("(t p) k -> p t k" if i < 2 else "(p t) k -> p t k", t=2)
                     tile_rows = raw_tile[:].rearrange("p (t k) -> p t k", t=2)
                     if slab > 0:
                         nc.sync.dma_start(out=tile_rows, in_=rows)
@@ -104,14 +108,15 @@ def tile_gcnlayer_pa_k_kernel(tc, h1, adj, W2, b2, out):
                                 nc.sync.dma_start(out=dst[:, :, cols], in_=src_rows[:, :, cols])
                 else:
                     m, q = divmod(n - LOADS_A, TILE_LOADS)
-                    a = HALF_TILES + m
+                    pair, odd = divmod(HALF_TILES + m, 2)
+                    nodes = h1[pair * 2 * P : (pair + 1) * 2 * P, q * RAW_K : (q + 1) * RAW_K]
                     nc.sync.dma_start(
-                        out=raw_tile[:], in_=h1[a * P : (a + 1) * P, q * RAW_K : (q + 1) * RAW_K]
+                        out=raw_tile[:], in_=nodes.rearrange("(p e) k -> p e k", e=2)[:, odd, :]
                     )
                 for b in ADJ_LOADS.get(n + 1, ()):
                     nc.sync.dma_start(out=adj_sb[:, b, :], in_=adj[b * P : (b + 1) * P, :])
-                if n + 1 == LOADS_A:
-                    nc.sync.dma_start(out=bias_bc[:], in_=b2.partition_broadcast(P))
+                if n + 1 == SLAB_LOADS:
+                    nc.sync.dma_start(out=bias_row[0:1, :], in_=b2.rearrange("(o f) -> o f", o=1))
 
         def copy_out(on_vector, dst, src):
             if on_vector:
@@ -144,6 +149,11 @@ def tile_gcnlayer_pa_k_kernel(tc, h1, adj, W2, b2, out):
             x_codes = stage.tile([P, PACK * P], U32, tag="x_codes", align_bytes=64)
             x_scales = stage.tile([P, PACK * P], U8, tag="x_scales", align_bytes=64)
             return x_codes, x_scales
+
+        def spread_bias():
+            bank = tr_psum.tile([P, OUT_F], F32, tag="bank")
+            nc.tensor.matmul(bank[:], lhsT=ones[:], rhs=bias_row[:], start=True, stop=True)
+            nc.scalar.copy(out=bias_bc[:], in_=bank[:])
 
         acc = {}
 
@@ -206,13 +216,16 @@ def tile_gcnlayer_pa_k_kernel(tc, h1, adj, W2, b2, out):
             an_rows[a] = rows
 
         def adj_transpose(a):
-            an_t = acc_psum.tile([P, NODE_TILES, P], BF16, tag="acc")
-            for jt in range(NODE_TILES):
-                nc.tensor.transpose(an_t[:, jt, :], an_rows[a][:, jt * P : (jt + 1) * P], ident_bf16[:])
+            an_t = acc_psum.tile([P, NODE_PASSES, 2, P], F32, tag="acc")
+            words = an_rows[a][:].bitcast(F32)
+            for g in range(NODE_PASSES):
+                for u in range(2):
+                    col = g * UNIT_WORDS + u * P
+                    nc.tensor.transpose(an_t[:, g, u, :], words[:, col : col + P], ident_f32[:])
             grouped = stage.tile([P, NODE_PASSES * K_PASS], BF16, tag="an_grouped", align_bytes=64)
             nc.scalar.copy(
-                out=grouped[:].rearrange("p (g i t) -> p g i t", g=NODE_PASSES, t=PACK),
-                in_=an_t[:].rearrange("p (g t) i -> p g i t", t=PACK),
+                out=grouped[:].bitcast(F32).rearrange("p (g i u) -> p g i u", g=NODE_PASSES, u=2),
+                in_=an_t[:].rearrange("p g u i -> p g i u"),
             )
             an_grouped[a] = grouped
 
@@ -229,6 +242,8 @@ def tile_gcnlayer_pa_k_kernel(tc, h1, adj, W2, b2, out):
             sums_adj = c >= ADJ_SUM_ROUNDS
             w_grouped = transpose_four_units(w_units, (False, sums_adj))
             x_grouped = transpose_four_units(x_units, (False, True))
+            if c == SLAB_PASSES:
+                spread_bias()
             quantise(w_grouped[:], w_codes[:, c, :], w_scales[:, c, :])
             x_codes, x_scales = new_x_codes()
             quantise(x_grouped[:], x_codes[:], x_scales[:])

@@ -27,7 +27,7 @@ RAW_K = RAW_UNITS * K_PASS
 SLAB_PASSES = 2
 SLAB_K = SLAB_PASSES * K_PASS
 SLAB_LOADS = 4
-RAW_BUFS = 20
+RAW_BUFS = 16
 ROUNDS_A = PASSES
 ROUNDS = ROUNDS_A + 2 * HALF_TILES
 LOADS_A = SLAB_LOADS * PASSES // SLAB_PASSES
@@ -35,7 +35,7 @@ TILE_LOADS = PASSES // RAW_UNITS
 LOADS = LOADS_A + HALF_TILES * TILE_LOADS
 ADJ_LOADS = {20: (0,), 22: (1,), 24: (2,), 26: (3,), 28: (4,), 30: (5,), 32: (6, 7)}
 ADJ_SUM_ROUNDS = 8
-AN_SCALED = ((), (), (0,), (1, 2), (3,), (4, 5), (6, 7), ())
+AN_SCALED = ((), (), (0,), (1, 2), (3, 4), (5,), (6, 7), ())
 
 FLOPS = 2 * NODES * HID * OUT_F + 2 * NODES * NODES * OUT_F
 
@@ -48,12 +48,10 @@ def tile_gcnlayer_pa_k_kernel(tc, h1, adj, W2, b2, out):
         raw_pool = ctx.enter_context(tc.tile_pool(name="raw", bufs=RAW_BUFS))
         stage = ctx.enter_context(tc.tile_pool(name="stage", bufs=4))
         tr_psum = ctx.enter_context(tc.psum_pool(name="tr_psum", bufs=4))
-        acc_psum = ctx.enter_context(tc.psum_pool(name="acc_psum", bufs=4))
+        acc_psum = ctx.enter_context(tc.psum_pool(name="acc_psum", bufs=1))
 
         ident_f32 = keep.tile([P, P], F32)
         make_identity(nc, ident_f32[:])
-        ident_bf16 = keep.tile([P, P], BF16)
-        make_identity(nc, ident_bf16[:])
 
         one = keep.tile([P, 1], F32)
         nc.vector.memset(one[:], 1.0)
@@ -71,9 +69,7 @@ def tile_gcnlayer_pa_k_kernel(tc, h1, adj, W2, b2, out):
         h_grouped = keep.tile([P, NODE_PASSES, OUT_F * PACK], BF16, align_bytes=64)
         h_codes = keep.tile([P, NODE_PASSES, OUT_F], U32, align_bytes=64)
         h_scales = keep.tile([P, NODE_PASSES, OUT_F], U8, align_bytes=64)
-        adj_sb = keep.tile([P, NODE_TILES, NODES], BF16)
-        adj_copy = keep.tile([P, NODES], BF16)
-        diag = keep.tile([P, NODE_TILES, P], F32)
+        a_f32 = keep.tile([P, NODE_TILES, NODES], F32)
         adj_sum = keep.tile([P, NODE_TILES], F32)
         deg = keep.tile([P, NODE_TILES], F32)
         root = keep.tile([P, NODE_TILES], F32)
@@ -85,6 +81,7 @@ def tile_gcnlayer_pa_k_kernel(tc, h1, adj, W2, b2, out):
         an_scales = keep.tile([P, NODE_TILES, NODE_PASSES * P], U8, align_bytes=64)
 
         raw = []
+        adj_tiles = []
         first_slab = []
 
         def load_to(end):
@@ -114,7 +111,9 @@ def tile_gcnlayer_pa_k_kernel(tc, h1, adj, W2, b2, out):
                         out=raw_tile[:], in_=nodes.rearrange("(p e) k -> p e k", e=2)[:, odd, :]
                     )
                 for b in ADJ_LOADS.get(n + 1, ()):
-                    nc.sync.dma_start(out=adj_sb[:, b, :], in_=adj[b * P : (b + 1) * P, :])
+                    adj_raw = raw_pool.tile([P, NODES], BF16, tag="adj", bufs=NODE_TILES)
+                    nc.sync.dma_start(out=adj_raw[:], in_=adj[b * P : (b + 1) * P, :])
+                    adj_tiles.append(adj_raw)
                 if n + 1 == SLAB_LOADS:
                     nc.sync.dma_start(out=bias_row[0:1, :], in_=b2.rearrange("(o f) -> o f", o=1))
 
@@ -160,7 +159,10 @@ def tile_gcnlayer_pa_k_kernel(tc, h1, adj, W2, b2, out):
         def run_passes(passes, f0=0, width=OUT_F):
             for m, c, x_codes, x_scales in passes:
                 if c == 0:
-                    acc[m, f0] = acc_psum.tile([P, width], F32, tag="acc", name="acc%d_%d" % (m, f0))
+                    bank = m if m < HALF_TILES else (m + f0 // HALF_F) % 2
+                    acc[m, f0] = acc_psum.tile(
+                        [P, width], F32, tag="acc%d" % bank, name="acc%d_%d" % (m, f0)
+                    )
                 nc.tensor.matmul_mx(
                     out=acc[m, f0][:],
                     lhsT=x_codes.bitcast(FP8X4),
@@ -196,27 +198,23 @@ def tile_gcnlayer_pa_k_kernel(tc, h1, adj, W2, b2, out):
 
         def adj_row_sum(a):
             nc.scalar.activation(
-                out=adj_copy[:], in_=adj_sb[:, a, :], func=ACT.Copy, accum_out=adj_sum[:, a : a + 1]
+                out=a_f32[:, a, :], in_=adj_tiles[a][:], func=ACT.Copy, accum_out=adj_sum[:, a : a + 1]
             )
-            nc.vector.tensor_tensor(
-                out=diag[:, a, :], in0=adj_sb[:, a, a * P : (a + 1) * P], in1=ident_bf16[:], op=ALU.add
-            )
+
+        def adj_self_loops(a):
+            block = a_f32[:, a, a * P : (a + 1) * P]
+            nc.vector.tensor_tensor(out=block, in0=block, in1=ident_f32[:], op=ALU.add)
 
         def adj_scale(a):
             rows = stage.tile([P, NODES], BF16, tag="an_rows")
-            block = slice(a * P, (a + 1) * P)
             nc.vector.scalar_tensor_tensor(
-                out=rows[:], in0=adj_sb[:, a, :], scalar=r[:, a : a + 1], in1=r_bc[:],
-                op0=ALU.mult, op1=ALU.mult,
-            )
-            nc.vector.scalar_tensor_tensor(
-                out=rows[:, block], in0=diag[:, a, :], scalar=r[:, a : a + 1], in1=r_bc[:, block],
+                out=rows[:], in0=a_f32[:, a, :], scalar=r[:, a : a + 1], in1=r_bc[:],
                 op0=ALU.mult, op1=ALU.mult,
             )
             an_rows[a] = rows
 
         def adj_transpose(a):
-            an_t = acc_psum.tile([P, NODE_PASSES, 2, P], F32, tag="acc")
+            an_t = acc_psum.tile([P, NODE_PASSES, 2, P], F32, tag="acc%d" % (2 + a % 2))
             words = an_rows[a][:].bitcast(F32)
             for g in range(NODE_PASSES):
                 for u in range(2):
@@ -249,6 +247,8 @@ def tile_gcnlayer_pa_k_kernel(tc, h1, adj, W2, b2, out):
             quantise(x_grouped[:], x_codes[:], x_scales[:])
             if sums_adj:
                 adj_row_sum(c - ADJ_SUM_ROUNDS)
+            if c > ADJ_SUM_ROUNDS:
+                adj_self_loops(c - ADJ_SUM_ROUNDS - 1)
             run_passes(waiting)
             waiting = []
             for m in range(HALF_TILES):
@@ -286,6 +286,7 @@ def tile_gcnlayer_pa_k_kernel(tc, h1, adj, W2, b2, out):
             to_pack = AN_SCALED[i - ROUNDS_A - 1] if i > ROUNDS_A else ()
             if i == ROUNDS_A:
                 degrees_to_r()
+                adj_self_loops(LAST)
             grouped = []
             for call in range(2):
                 units = [(raw[used + call], n) for n in range(RAW_UNITS)]
@@ -342,7 +343,7 @@ def tile_gcnlayer_pa_k_kernel(tc, h1, adj, W2, b2, out):
                 if a < HALF_TILES:
                     out_sum = tr_psum.tile([P, HALF_F], F32, tag="bank")
                 else:
-                    out_sum = acc_psum.tile([P, HALF_F], F32, tag="acc")
+                    out_sum = acc_psum.tile([P, HALF_F], F32, tag="acc%d" % (NODE_TILES - 1 - a))
                 out_sums.append(out_sum)
                 for g in range(NODE_PASSES):
                     cols = slice(g * P, (g + 1) * P)

@@ -179,10 +179,11 @@ def tile_gcnlayer_pa_k_kernel(tc, h1, adj, W2, b2, out):
                 out=h_bf16[:, m, features], in0=acc[m, f0][:], in1=bias_bc[:, features], op=ALU.add
             )
 
-        def group_h(g, f0=0, width=OUT_F):
-            nc.vector.tensor_copy(
-                out=h_grouped[:, g, PACK * f0 : PACK * (f0 + width)].rearrange("p (f t) -> p f t", t=PACK),
-                in_=h_bf16[:, PACK * g : PACK * (g + 1), f0 : f0 + width].rearrange("p t f -> p f t"),
+        def group_h(g, f0, width, on_vector):
+            copy_out(
+                on_vector,
+                h_grouped[:, g, PACK * f0 : PACK * (f0 + width)].rearrange("p (f t) -> p f t", t=PACK),
+                h_bf16[:, PACK * g : PACK * (g + 1), f0 : f0 + width].rearrange("p t f -> p f t"),
             )
 
         def quantise_h(g, f0=0, width=OUT_F):
@@ -319,17 +320,17 @@ def tile_gcnlayer_pa_k_kernel(tc, h1, adj, W2, b2, out):
                     h_from_sums(done)
             elif i % 2 == 0:
                 h_from_sums(m - 1)
-            if i == ROUNDS_A + 1:
-                group_h(0)
-            elif i == ROUNDS_A + 2:
-                quantise_h(0)
+
+        for f0 in (0, HALF_F):
+            group_h(0, f0, HALF_F, False)
 
         run_passes(waiting, 0, HALF_F)
         run_passes(last_passes, HALF_F, HALF_F)
 
         for f0 in (0, HALF_F):
             h_from_sums(LAST, f0, HALF_F)
-            group_h(1, f0, HALF_F)
+            group_h(1, f0, HALF_F, True)
+            quantise_h(0, f0, HALF_F)
             quantise_h(1, f0, HALF_F)
 
         out_sb = []

@@ -29,13 +29,14 @@ SLAB_K = SLAB_PASSES * K_PASS
 SLAB_LOADS = 4
 RAW_BUFS = 16
 ROUNDS_A = PASSES
-ROUNDS = ROUNDS_A + 2 * HALF_TILES
+ROUND_LOADS = (2, 2, 3, 3, 3, 3)
+WIDE_ROUND = 2
 LOADS_A = SLAB_LOADS * PASSES // SLAB_PASSES
 TILE_LOADS = PASSES // RAW_UNITS
 LOADS = LOADS_A + HALF_TILES * TILE_LOADS
 ADJ_LOADS = {20: (0,), 22: (1,), 24: (2,), 26: (3,), 28: (4,), 30: (5,), 32: (6, 7)}
 ADJ_SUM_ROUNDS = 8
-AN_SCALED = ((), (), (0,), (1, 2), (3, 4), (5,), (6, 7), ())
+AN_SCALED = ((), (0,), (1, 2, 3), (4, 5), (6, 7), ())
 
 FLOPS = 2 * NODES * HID * OUT_F + 2 * NODES * NODES * OUT_F
 
@@ -47,8 +48,17 @@ def tile_gcnlayer_pa_k_kernel(tc, h1, adj, W2, b2, out):
         keep = ctx.enter_context(tc.tile_pool(name="keep", bufs=1))
         raw_pool = ctx.enter_context(tc.tile_pool(name="raw", bufs=RAW_BUFS))
         stage = ctx.enter_context(tc.tile_pool(name="stage", bufs=4))
-        tr_psum = ctx.enter_context(tc.psum_pool(name="tr_psum", bufs=4))
-        acc_psum = ctx.enter_context(tc.psum_pool(name="acc_psum", bufs=1))
+        psum = ctx.enter_context(tc.psum_pool(name="psum", bufs=1))
+        transpose_banks = [4, 5, 6, 7]
+
+        def bank_tile(bank, shape, what):
+            return psum.tile(shape, F32, tag="bank%d" % bank, name=what)
+
+        def next_bank(shape, what):
+            bank = transpose_banks.pop(0)
+            transpose_banks.append(bank)
+            return bank_tile(bank, shape, what)
+
 
         ident_f32 = keep.tile([P, P], F32)
         make_identity(nc, ident_f32[:])
@@ -127,7 +137,7 @@ def tile_gcnlayer_pa_k_kernel(tc, h1, adj, W2, b2, out):
             grouped = stage.tile([P, PACK * K_PASS], BF16, tag="grouped", align_bytes=64)
             grouped_words = grouped[:].bitcast(F32).rearrange("p (n r u) -> p n r u", n=4, u=2)
             for b in range(2):
-                bank = tr_psum.tile([P, 2, 2, P], F32, tag="bank")
+                bank = next_bank([P, 2, 2, P], "units")
                 for n in range(2):
                     raw_tile, unit = units[2 * b + n]
                     words = raw_tile[:].bitcast(F32)
@@ -145,12 +155,12 @@ def tile_gcnlayer_pa_k_kernel(tc, h1, adj, W2, b2, out):
             nc.vector.quantize_mx(out=codes.bitcast(FP8X4), scales=scales, in_=grouped)
 
         def new_x_codes():
-            x_codes = stage.tile([P, PACK * P], U32, tag="x_codes", align_bytes=64)
-            x_scales = stage.tile([P, PACK * P], U8, tag="x_scales", align_bytes=64)
+            x_codes = stage.tile([P, PACK * P], U32, tag="x_codes", align_bytes=64, bufs=6)
+            x_scales = stage.tile([P, PACK * P], U8, tag="x_scales", align_bytes=64, bufs=6)
             return x_codes, x_scales
 
         def spread_bias():
-            bank = tr_psum.tile([P, OUT_F], F32, tag="bank")
+            bank = next_bank([P, OUT_F], "bias")
             nc.tensor.matmul(bank[:], lhsT=ones[:], rhs=bias_row[:], start=True, stop=True)
             nc.scalar.copy(out=bias_bc[:], in_=bank[:])
 
@@ -160,9 +170,7 @@ def tile_gcnlayer_pa_k_kernel(tc, h1, adj, W2, b2, out):
             for m, c, x_codes, x_scales in passes:
                 if c == 0:
                     bank = m if m < HALF_TILES else (m + f0 // HALF_F) % 2
-                    acc[m, f0] = acc_psum.tile(
-                        [P, width], F32, tag="acc%d" % bank, name="acc%d_%d" % (m, f0)
-                    )
+                    acc[m, f0] = bank_tile(bank, [P, width], "acc%d_%d" % (m, f0))
                 nc.tensor.matmul_mx(
                     out=acc[m, f0][:],
                     lhsT=x_codes.bitcast(FP8X4),
@@ -215,7 +223,7 @@ def tile_gcnlayer_pa_k_kernel(tc, h1, adj, W2, b2, out):
             an_rows[a] = rows
 
         def adj_transpose(a):
-            an_t = acc_psum.tile([P, NODE_PASSES, 2, P], F32, tag="acc%d" % (2 + a % 2))
+            an_t = next_bank([P, NODE_PASSES, 2, P], "an_t")
             words = an_rows[a][:].bitcast(F32)
             for g in range(NODE_PASSES):
                 for u in range(2):
@@ -269,7 +277,7 @@ def tile_gcnlayer_pa_k_kernel(tc, h1, adj, W2, b2, out):
 
         def spread_r():
             for half in range(2):
-                bank = tr_psum.tile([P, PACK, P], F32, tag="bank")
+                bank = next_bank([P, PACK, P], "r_spread")
                 for q in range(PACK):
                     a = PACK * half + q
                     nc.tensor.transpose(bank[:, q, :], r[:, a : a + 1].to_broadcast([P, P]), ident_f32[:])
@@ -279,47 +287,50 @@ def tile_gcnlayer_pa_k_kernel(tc, h1, adj, W2, b2, out):
                 )
 
         last_passes = []
-        for i in range(ROUNDS_A, ROUNDS):
-            used = LOADS_A + 2 * (i - ROUNDS_A)
+        used = LOADS_A
+        for i in range(len(ROUND_LOADS)):
             load_to(used + RAW_BUFS)
-            m = (i - ROUNDS_A) // 2 + HALF_TILES
-            to_scale = AN_SCALED[i - ROUNDS_A]
-            to_pack = AN_SCALED[i - ROUNDS_A - 1] if i > ROUNDS_A else ()
-            if i == ROUNDS_A:
+            to_scale = AN_SCALED[i]
+            to_pack = AN_SCALED[i - 1] if i > 0 else ()
+            if i == 0:
                 degrees_to_r()
                 adj_self_loops(LAST)
+            if i == WIDE_ROUND:
+                transpose_banks.extend((2, 3))
             grouped = []
-            for call in range(2):
-                units = [(raw[used + call], n) for n in range(RAW_UNITS)]
-                grouped.append(transpose_four_units(units, (False, False)))
-            if i == ROUNDS_A + 1:
+            for load in range(used, used + ROUND_LOADS[i]):
+                units = [(raw[load], n) for n in range(RAW_UNITS)]
+                grouped.append((load, transpose_four_units(units, (False, False))))
+            if i == 1:
                 spread_r()
             for a in to_pack:
                 adj_transpose(a)
             fresh = []
-            for call in range(2):
+            for n, (load, load_grouped) in enumerate(grouped):
+                m, q = divmod(load - LOADS_A, TILE_LOADS)
                 x_codes, x_scales = new_x_codes()
-                quantise(grouped[call][:], x_codes[:], x_scales[:])
-                for n in range(PACK):
-                    cols = slice(n * P, (n + 1) * P)
-                    c = (i % 2) * 2 * PACK + PACK * call + n
-                    fresh.append((m, c, x_codes[:, cols], x_scales[:, cols]))
-                if call == 0:
-                    for a in to_scale:
-                        adj_scale(a)
+                quantise(load_grouped[:], x_codes[:], x_scales[:])
+                for unit in range(RAW_UNITS):
+                    cols = slice(unit * P, (unit + 1) * P)
+                    c = q * RAW_UNITS + unit
+                    fresh.append((HALF_TILES + m, c, x_codes[:, cols], x_scales[:, cols]))
+                for a in to_scale[n : n + 1]:
+                    adj_scale(a)
             for a in to_pack:
                 adj_quantise(a)
-            if i < ROUNDS - 1:
-                run_passes(waiting)
+            run_passes([entry for entry in waiting if entry[0] < LAST])
+            last = [entry for entry in waiting if entry[0] == LAST]
+            run_passes(last, 0, HALF_F)
+            last_passes.extend(last)
+            if i == 0:
+                closed = range(HALF_TILES)
             else:
-                last_passes = waiting + fresh
-                run_passes(waiting, 0, HALF_F)
+                closed = [m for m, c, codes, scales in waiting if c == PASSES - 1]
+            for m in closed:
+                h_from_sums(m)
             waiting = fresh
-            if i == ROUNDS_A:
-                for done in range(HALF_TILES):
-                    h_from_sums(done)
-            elif i % 2 == 0:
-                h_from_sums(m - 1)
+            used += ROUND_LOADS[i]
+        last_passes.extend(waiting)
 
         for f0 in (0, HALF_F):
             group_h(0, f0, HALF_F, False)
@@ -341,10 +352,7 @@ def tile_gcnlayer_pa_k_kernel(tc, h1, adj, W2, b2, out):
             features = slice(f0, f0 + HALF_F)
             out_sums = []
             for a in range(NODE_TILES):
-                if a < HALF_TILES:
-                    out_sum = tr_psum.tile([P, HALF_F], F32, tag="bank")
-                else:
-                    out_sum = acc_psum.tile([P, HALF_F], F32, tag="acc%d" % (NODE_TILES - 1 - a))
+                out_sum = bank_tile(NODE_TILES - 1 - a, [P, HALF_F], "out%d_%d" % (a, f0))
                 out_sums.append(out_sum)
                 for g in range(NODE_PASSES):
                     cols = slice(g * P, (g + 1) * P)

from contextlib import ExitStack

import concourse.mybir as mybir
from concourse.masks import make_identity

F32 = mybir.dt.float32
BF16 = mybir.dt.bfloat16
U32 = mybir.dt.uint32
U8 = mybir.dt.uint8
FP8X4 = mybir.dt.float8_e4m3fn_x4
ACT = mybir.ActivationFunctionType
ALU = mybir.AluOpType

P = 128
PACK = 4
K_PASS = P * PACK
NODES, HID, OUT_F = 1024, 8192, 512
PASSES = HID // K_PASS
NODE_TILES = NODES // P
NODE_PASSES = NODES // K_PASS
HALF_TILES = NODE_TILES // 2
HALF_F = OUT_F // 2
LAST = NODE_TILES - 1
UNIT_WORDS = K_PASS // 2
RAW_UNITS = 4
RAW_K = RAW_UNITS * K_PASS
SLAB_PASSES = 2
SLAB_K = SLAB_PASSES * K_PASS
SLAB_LOADS = 4
RAW_BUFS = 16
ROUNDS_A = PASSES
ROUND_LOADS = (2, 2, 3, 3, 3, 3)
WIDE_ROUND = 2
LOADS_A = SLAB_LOADS * PASSES // SLAB_PASSES
TILE_LOADS = PASSES // RAW_UNITS
LOADS = LOADS_A + HALF_TILES * TILE_LOADS
ADJ_LOADS = {20: (0,), 22: (1,), 24: (2,), 26: (3,), 28: (4,), 30: (5,), 32: (6, 7)}
ADJ_SUM_ROUNDS = 8
AN_SCALED = ((), (0,), (1, 2, 3), (4, 5), (6, 7), ())

FLOPS = 2 * NODES * HID * OUT_F + 2 * NODES * NODES * OUT_F


def tile_gcnlayer_pa_k_kernel(tc, h1, adj, W2, b2, out):
    nc = tc.nc
    with ExitStack() as ctx:
        ctx.enter_context(tc.manual_schedule())
        keep = ctx.enter_context(tc.tile_pool(name="keep", bufs=1))
        raw_pool = ctx.enter_context(tc.tile_pool(name="raw", bufs=RAW_BUFS))
        stage = ctx.enter_context(tc.tile_pool(name="stage", bufs=4))
        psum = ctx.enter_context(tc.psum_pool(name="psum", bufs=1))
        transpose_banks = [4, 5, 6, 7]

        def bank_tile(bank, shape, what):
            return psum.tile(shape, F32, tag="bank%d" % bank, name=what)

        def next_bank(shape, what):
            bank = transpose_banks.pop(0)
            transpose_banks.append(bank)
            return bank_tile(bank, shape, what)


        ident_f32 = keep.tile([P, P], F32)
        make_identity(nc, ident_f32[:])

        one = keep.tile([P, 1], F32)
        nc.vector.memset(one[:], 1.0)
        one_root = keep.tile([P, 1], F32)
        nc.scalar.activation(out=one_root[:], in_=one[:], func=ACT.Sqrt)

        w_codes = keep.tile([P, PASSES, OUT_F], U32, align_bytes=64)
        w_scales = keep.tile([P, PASSES, OUT_F], U8, align_bytes=64)
        bias_row = keep.tile([P, OUT_F], BF16)
        nc.vector.memset(bias_row[:], 0.0)
        ones = keep.tile([P, P], BF16)
        nc.vector.memset(ones[:], 1.0)
        bias_bc = keep.tile([P, OUT_F], F32)
        h_bf16 = keep.tile([P, NODE_TILES, OUT_F], BF16)
        h_grouped = keep.tile([P, NODE_PASSES, OUT_F * PACK], BF16, align_bytes=64)
        h_codes = keep.tile([P, NODE_PASSES, OUT_F], U32, align_bytes=64)
        h_scales = keep.tile([P, NODE_PASSES, OUT_F], U8, align_bytes=64)
        a_f32 = keep.tile([P, NODE_TILES, NODES], F32)
        adj_sum = keep.tile([P, NODE_TILES], F32)
        deg = keep.tile([P, NODE_TILES], F32)
        root = keep.tile([P, NODE_TILES], F32)
        r_first = keep.tile([P, NODE_TILES], F32)
        deg_rr = keep.tile([P, NODE_TILES], F32)
        r = keep.tile([P, NODE_TILES], F32)
        r_bc = keep.tile([P, NODES], F32)
        an_codes = keep.tile([P, NODE_TILES, NODE_PASSES * P], U32, align_bytes=64)
        an_scales = keep.tile([P, NODE_TILES, NODE_PASSES * P], U8, align_bytes=64)

        raw = []
        adj_tiles = []
        first_slab = []

        def load_to(end):
            for n in range(len(raw), min(end, LOADS)):
                raw_tile = raw_pool.tile([P, RAW_K], BF16, tag="raw")
                raw.append(raw_tile)
                if n < LOADS_A:
                    slab, i = divmod(n, SLAB_LOADS)
                    src, a = (W2, 2 * i) if i < 2 else (h1, 2 * (i - 2))
                    rows = src[a * P : (a + 2) * P, slab * SLAB_K : (slab + 1) * SLAB_K]
                    rows = rows.rearrange("(t p) k -> p t k" if i < 2 else "(p t) k -> p t k", t=2)
                    tile_rows = raw_tile[:].rearrange("p (t k) -> p t k", t=2)
                    if slab > 0:
                        nc.sync.dma_start(out=tile_rows, in_=rows)
                    else:
                        first_slab.append((tile_rows, rows))
                    if n == SLAB_LOADS - 1:
                        for c in range(SLAB_PASSES):
                            cols = slice(c * K_PASS, (c + 1) * K_PASS)
                            for dst, src_rows in first_slab:
                                nc.sync.dma_start(out=dst[:, :, cols], in_=src_rows[:, :, cols])
                else:
                    m, q = divmod(n - LOADS_A, TILE_LOADS)
                    pair, odd = divmod(HALF_TILES + m, 2)
                    nodes = h1[pair * 2 * P : (pair + 1) * 2 * P, q * RAW_K : (q + 1) * RAW_K]
                    nc.sync.dma_start(
                        out=raw_tile[:], in_=nodes.rearrange("(p e) k -> p e k", e=2)[:, odd, :]
                    )
                for b in ADJ_LOADS.get(n + 1, ()):
                    adj_raw = raw_pool.tile([P, NODES], BF16, tag="adj", bufs=NODE_TILES)
                    nc.sync.dma_start(out=adj_raw[:], in_=adj[b * P : (b + 1) * P, :])
                    adj_tiles.append(adj_raw)
                if n + 1 == SLAB_LOADS:
                    nc.sync.dma_start(out=bias_row[0:1, :], in_=b2.rearrange("(o f) -> o f", o=1))

        def copy_out(on_vector, dst, src):
            if on_vector:
                nc.vector.tensor_copy(out=dst, in_=src)
            else:
                nc.scalar.copy(out=dst, in_=src)

        def transpose_four_units(units, bank_on_vector):
            grouped = stage.tile([P, PACK * K_PASS], BF16, tag="grouped", align_bytes=64)
            grouped_words = grouped[:].bitcast(F32).rearrange("p (n r u) -> p n r u", n=4, u=2)
            for b in range(2):
                bank = next_bank([P, 2, 2, P], "units")
                for n in range(2):
                    raw_tile, unit = units[2 * b + n]
                    words = raw_tile[:].bitcast(F32)
                    for u in range(2):
                        col = unit * UNIT_WORDS + u * P
                        nc.tensor.transpose(bank[:, n, u, :], words[:, col : col + P], ident_f32[:])
                copy_out(
                    bank_on_vector[b],
                    grouped_words[:, 2 * b : 2 * b + 2],
                    bank[:].rearrange("p n u r -> p n r u"),
                )
            return grouped

        def quantise(grouped, codes, scales):
            nc.vector.quantize_mx(out=codes.bitcast(FP8X4), scales=scales, in_=grouped)

        def new_x_codes():
            x_codes = stage.tile([P, PACK * P], U32, tag="x_codes", align_bytes=64, bufs=6)
            x_scales = stage.tile([P, PACK * P], U8, tag="x_scales", align_bytes=64, bufs=6)
            return x_codes, x_scales

        def spread_bias():
            bank = next_bank([P, OUT_F], "bias")
            nc.tensor.matmul(bank[:], lhsT=ones[:], rhs=bias_row[:], start=True, stop=True)
            nc.scalar.copy(out=bias_bc[:], in_=bank[:])

        acc = {}

        def run_passes(passes, f0=0, width=OUT_F):
            for m, c, x_codes, x_scales in passes:
                if c == 0:
                    bank = m if m < HALF_TILES else (m + f0 // HALF_F) % 2
                    acc[m, f0] = bank_tile(bank, [P, width], "acc%d_%d" % (m, f0))
                nc.tensor.matmul_mx(
                    out=acc[m, f0][:],
                    lhsT=x_codes.bitcast(FP8X4),
                    lhsT_scale=x_scales,
                    rhs=w_codes[:, c, f0 : f0 + width].bitcast(FP8X4),
                    rhs_scale=w_scales[:, c, f0 : f0 + width],
                    start=(c == 0),
                    stop=(c == PASSES - 1),
                )

        def h_from_sums(m, f0=0, width=OUT_F):
            features = slice(f0, f0 + width)
            nc.vector.tensor_tensor(
                out=h_bf16[:, m, features], in0=acc[m, f0][:], in1=bias_bc[:, features], op=ALU.add
            )

        def group_h(g, f0, width, on_vector):
            copy_out(
                on_vector,
                h_grouped[:, g, PACK * f0 : PACK * (f0 + width)].rearrange("p (f t) -> p f t", t=PACK),
                h_bf16[:, PACK * g : PACK * (g + 1), f0 : f0 + width].rearrange("p t f -> p f t"),
            )

        def quantise_h(g, f0=0, width=OUT_F):
            features = slice(f0, f0 + width)
            quantise(
                h_grouped[:, g, PACK * f0 : PACK * (f0 + width)],
                h_codes[:, g, features],
                h_scales[:, g, features],
            )

        an_rows = {}
        an_grouped = {}

        def adj_row_sum(a):
            nc.scalar.activation(
                out=a_f32[:, a, :], in_=adj_tiles[a][:], func=ACT.Copy, accum_out=adj_sum[:, a : a + 1]
            )

        def adj_self_loops(a):
            block = a_f32[:, a, a * P : (a + 1) * P]
            nc.vector.tensor_tensor(out=block, in0=block, in1=ident_f32[:], op=ALU.add)

        def adj_scale(a):
            rows = stage.tile([P, NODES], BF16, tag="an_rows")
            nc.vector.scalar_tensor_tensor(
                out=rows[:], in0=a_f32[:, a, :], scalar=r[:, a : a + 1], in1=r_bc[:],
                op0=ALU.mult, op1=ALU.mult,
            )
            an_rows[a] = rows

        def adj_transpose(a):
            an_t = next_bank([P, NODE_PASSES, 2, P], "an_t")
            words = an_rows[a][:].bitcast(F32)
            for g in range(NODE_PASSES):
                for u in range(2):
                    col = g * UNIT_WORDS + u * P
                    nc.tensor.transpose(an_t[:, g, u, :], words[:, col : col + P], ident_f32[:])
            grouped = stage.tile([P, NODE_PASSES * K_PASS], BF16, tag="an_grouped", align_bytes=64)
            nc.scalar.copy(
                out=grouped[:].bitcast(F32).rearrange("p (g i u) -> p g i u", g=NODE_PASSES, u=2),
                in_=an_t[:].rearrange("p g u i -> p g i u"),
            )
            an_grouped[a] = grouped

        def adj_quantise(a):
            quantise(an_grouped[a][:], an_codes[:, a, :], an_scales[:, a, :])

        waiting = []
        for c in range(ROUNDS_A):
            slab, in_slab = divmod(c, SLAB_PASSES)
            used = SLAB_LOADS * slab
            load_to(used + RAW_BUFS)
            w_units = [(raw[used + a // 2], SLAB_PASSES * (a % 2) + in_slab) for a in range(HALF_TILES)]
            x_units = [(raw[used + 2 + a // 2], SLAB_PASSES * (a % 2) + in_slab) for a in range(HALF_TILES)]
            sums_adj = c >= ADJ_SUM_ROUNDS
            w_grouped = transpose_four_units(w_units, (False, sums_adj))
            x_grouped = transpose_four_units(x_units, (False, True))
            if c == SLAB_PASSES:
                spread_bias()
            quantise(w_grouped[:], w_codes[:, c, :], w_scales[:, c, :])
            x_codes, x_scales = new_x_codes()
            quantise(x_grouped[:], x_codes[:], x_scales[:])
            if sums_adj:
                adj_row_sum(c - ADJ_SUM_ROUNDS)
            if c > ADJ_SUM_ROUNDS:
                adj_self_loops(c - ADJ_SUM_ROUNDS - 1)
            run_passes(waiting)
            waiting = []
            for m in range(HALF_TILES):
                cols = slice(m * P, (m + 1) * P)
                waiting.append((m, c, x_codes[:, cols], x_scales[:, cols]))

        def degrees_to_r():
            nc.vector.tensor_scalar_add(out=deg[:], in0=adj_sum[:], scalar1=1.0)
            nc.scalar.activation(out=root[:], in_=deg[:], func=ACT.Sqrt)
            nc.vector.reciprocal(out=r_first[:], in_=root[:])
            nc.vector.tensor_tensor(out=deg_rr[:], in0=deg[:], in1=r_first[:], op=ALU.mult)
            nc.vector.tensor_tensor(out=deg_rr[:], in0=deg_rr[:], in1=r_first[:], op=ALU.mult)
            nc.vector.tensor_scalar(
                out=deg_rr[:], in0=deg_rr[:], scalar1=-0.5, scalar2=1.5, op0=ALU.mult, op1=ALU.add
            )
            nc.vector.tensor_tensor(out=r[:], in0=r_first[:], in1=deg_rr[:], op=ALU.mult)

        def spread_r():
            for half in range(2):
                bank = next_bank([P, PACK, P], "r_spread")
                for q in range(PACK):
                    a = PACK * half + q
                    nc.tensor.transpose(bank[:, q, :], r[:, a : a + 1].to_broadcast([P, P]), ident_f32[:])
                nc.scalar.copy(
                    out=r_bc[:, half * K_PASS : (half + 1) * K_PASS],
                    in_=bank[:].rearrange("p q c -> p (q c)"),
                )

        last_passes = []
        used = LOADS_A
        for i in range(len(ROUND_LOADS)):
            load_to(used + RAW_BUFS)
            to_scale = AN_SCALED[i]
            to_pack = AN_SCALED[i - 1] if i > 0 else ()
            if i == 0:
                degrees_to_r()
                adj_self_loops(LAST)
            if i == WIDE_ROUND:
                transpose_banks.extend((2, 3))
            grouped = []
            for load in range(used, used + ROUND_LOADS[i]):
                units = [(raw[load], n) for n in range(RAW_UNITS)]
                grouped.append((load, transpose_four_units(units, (False, False))))
            if i == 1:
                spread_r()
            for a in to_pack:
                adj_transpose(a)
            fresh = []
            for n, (load, load_grouped) in enumerate(grouped):
                m, q = divmod(load - LOADS_A, TILE_LOADS)
                x_codes, x_scales = new_x_codes()
                quantise(load_grouped[:], x_codes[:], x_scales[:])
                for unit in range(RAW_UNITS):
                    cols = slice(unit * P, (unit + 1) * P)
                    c = q * RAW_UNITS + unit
                    fresh.append((HALF_TILES + m, c, x_codes[:, cols], x_scales[:, cols]))
                for a in to_scale[n : n + 1]:
                    adj_scale(a)
            for a in to_pack:
                adj_quantise(a)
            run_passes([entry for entry in waiting if entry[0] < LAST])
            last = [entry for entry in waiting if entry[0] == LAST]
            run_passes(last, 0, HALF_F)
            last_passes.extend(last)
            if i == 0:
                closed = range(HALF_TILES)
            else:
                closed = [m for m, c, codes, scales in waiting if c == PASSES - 1]
            for m in closed:
                h_from_sums(m)
            waiting = fresh
            used += ROUND_LOADS[i]
        last_passes.extend(waiting)

        for f0 in (0, HALF_F):
            group_h(0, f0, HALF_F, False)

        run_passes(waiting, 0, HALF_F)
        run_passes(last_passes, HALF_F, HALF_F)

        for f0 in (0, HALF_F):
            h_from_sums(LAST, f0, HALF_F)
            group_h(1, f0, HALF_F, True)
            quantise_h(0, f0, HALF_F)
            quantise_h(1, f0, HALF_F)

        out_sb = []
        for n in range(NODE_TILES // 2):
            out_pair = raw_pool.tile([P, 2, OUT_F], F32, tag="raw")
            out_sb.append(out_pair)
        for f0 in (0, HALF_F):
            features = slice(f0, f0 + HALF_F)
            out_sums = []
            for a in range(NODE_TILES):
                out_sum = bank_tile(NODE_TILES - 1 - a, [P, HALF_F], "out%d_%d" % (a, f0))
                out_sums.append(out_sum)
                for g in range(NODE_PASSES):
                    cols = slice(g * P, (g + 1) * P)
                    nc.tensor.matmul_mx(
                        out=out_sum[:],
                        lhsT=an_codes[:, a, cols].bitcast(FP8X4),
                        lhsT_scale=an_scales[:, a, cols],
                        rhs=h_codes[:, g, features].bitcast(FP8X4),
                        rhs_scale=h_scales[:, g, features],
                        start=(g == 0),
                        stop=(g == NODE_PASSES - 1),
                    )
            on_vector = (5, 6, 7) if f0 == 0 else (1, 3, 5, 7)
            for a in range(NODE_TILES):
                copy_out(a in on_vector, out_sb[a // 2][:, a % 2, features], out_sums[a][:])
                if a % 2 == 1:
                    nc.sync.dma_start(
                        out=out[(a - 1) * P : (a + 1) * P, features].rearrange("(t p) f -> p t f", p=P),
                        in_=out_sb[a // 2][:, :, features],
                    )
